import numpy as np
import ml_dtypes


def mxq(x, axis, fmt="e4m3"):
    dtype, down = {"e4m3": (ml_dtypes.float8_e4m3fn, 7), "e5m2": (ml_dtypes.float8_e5m2, 14)}[fmt]
    v = np.moveaxis(np.asarray(x, np.float32).astype(ml_dtypes.bfloat16).astype(np.float64), axis, -1)
    blocks = v.reshape(v.shape[:-1] + (-1, 32))
    amax = np.abs(blocks).max(-1, keepdims=True)
    byte = np.maximum(np.where(amax > 0, np.frexp(amax)[1] - 1 + 127, 0) - down, 1)
    scale = np.exp2(byte - 127.0)
    codes = (blocks / scale).astype(np.float32).astype(dtype).astype(np.float64)
    return np.moveaxis((codes * scale).reshape(v.shape), -1, axis)


BF16 = ml_dtypes.bfloat16


def bf(x):
    return np.asarray(x, np.float32).astype(BF16)


def f64(x):
    return np.asarray(x).astype(np.float64)


N, B, T, C, R, O, NC, H, W = 31, 128, 4, 256, 4, 512, 512, 16, 4
BN_EPS = 1e-5
L2_EPS = 1e-12


def setup_inputs():
    off = 1.5 * np.random.standard_normal((N, 1, O))
    sd = 0.3 + 0.6 * np.random.random_sample((N, 1, O))
    col = (0.5 + np.random.random_sample((N, 1, NC))) / np.sqrt(O)
    return {"emb": bf(off + sd * np.random.standard_normal((N, B, O))),
            "gamma": bf(1.0 + 0.1 * np.random.standard_normal((N, O))),
            "beta": bf(0.1 * np.random.standard_normal((N, O))),
            "fc1d": bf(col * np.random.standard_normal((N, O, NC)))}


def reference(emb, gamma, beta, fc1d):
    e = f64(emb)
    mean = e.mean(axis=1, keepdims=True)
    var = ((e - mean) ** 2).mean(axis=1, keepdims=True)
    bn = f64(gamma)[:, None, :] * (e - mean) / np.sqrt(var + BN_EPS) + f64(beta)[:, None, :]
    bnn = bn / np.maximum(np.sqrt((bn ** 2).sum(axis=-1, keepdims=True)), L2_EPS)
    fc = f64(fc1d)
    fcn = fc / np.maximum(np.sqrt((fc ** 2).sum(axis=1, keepdims=True)), L2_EPS)
    logits = mxq(bnn, 2, "e4m3") @ mxq(fcn, 1, "e4m3")
    return np.transpose(logits, (1, 0, 2))

@@ -1,0 +1,209 @@
+from contextlib import ExitStack
+
+import concourse.mybir as mybir
+from concourse.masks import make_identity
+
+FP8X4 = mybir.dt.float8_e4m3fn_x4
+BF16 = mybir.dt.bfloat16
+F32 = mybir.dt.float32
+U32 = mybir.dt.uint32
+U8 = mybir.dt.uint8
+ALU = mybir.AluOpType
+ACT = mybir.ActivationFunctionType
+AXIS = mybir.AxisListType
+
+P = 128
+PACK = 4
+BINS = 31
+SAMPLES = 128
+FEATURES = P * PACK
+CLASSES = 512
+CHUNKS = CLASSES // P
+BN_EPS = 1e-5
+L2_EPS_SQUARED = 1e-24
+GROUP = 4
+STORE_BINS = 4
+
+FLOPS = 2 * BINS * SAMPLES * FEATURES * CLASSES
+
+
+def tile_gmpahead_pb_kernel(tc, emb, gamma, beta, fc1d, out):
+    nc = tc.nc
+    with ExitStack() as ctx:
+        keep = ctx.enter_context(tc.tile_pool(name="keep", bufs=1))
+
+        ident_bf16 = keep.tile([P, P], BF16)
+        make_identity(nc, ident_bf16[:])
+        ident_f32 = keep.tile([P, P], F32)
+        make_identity(nc, ident_f32[:])
+
+        gamma_sb = keep.tile([P, BINS, PACK], BF16)
+        nc.scalar.dma_start(out=gamma_sb[:], in_=gamma.rearrange("n (p t) -> p n t", t=PACK))
+        beta_sb = keep.tile([P, BINS, PACK], BF16)
+        nc.scalar.dma_start(out=beta_sb[:], in_=beta.rearrange("n (p t) -> p n t", t=PACK))
+
+        emb_codes = keep.tile([P, BINS, SAMPLES], U32, align_bytes=64)
+        emb_scales = keep.tile([P, BINS, SAMPLES], U8, align_bytes=64)
+        fc_sb = keep.tile([P, BINS, PACK, CLASSES], BF16)
+
+        groups = [(n0, min(GROUP, BINS - n0)) for n0 in range(0, BINS, GROUP)]
+
+        with tc.tile_pool(name="emb_work", bufs=2) as work, tc.psum_pool(name="emb_psum", bufs=2) as psum:
+            emb_sb = work.tile([P, BINS, FEATURES], BF16, bufs=1)
+            for n0, gn in groups:
+                nc.sync.dma_start(
+                    out=emb_sb[:, n0 : n0 + gn, :], in_=emb[n0 : n0 + gn].rearrange("n b o -> b n o")
+                )
+            for n0 in range(0, BINS, 2):
+                gn = min(2, BINS - n0)
+                nc.sync.dma_start(
+                    out=fc_sb[:, n0 : n0 + gn].rearrange("p n t k -> p n (t k)"),
+                    in_=fc1d[n0 : n0 + gn].rearrange("n (p t) k -> p n (t k)", t=PACK),
+                )
+
+            for n0, gn in groups:
+                cols = gn * PACK
+                x_pairs = []
+                mean_var = work.tile([P, GROUP * PACK, 2], F32)
+                for h in range(0, gn, 2):
+                    x_t = psum.tile([P, 2, PACK, SAMPLES], BF16, bufs=4)
+                    x_pairs.append(x_t)
+                    for j in range(h, min(h + 2, gn)):
+                        by_t = emb_sb[:, n0 + j, :].rearrange("b (p t) -> b t p", t=PACK)
+                        for t in range(PACK):
+                            nc.tensor.transpose(x_t[:, j - h, t, :], by_t[:, t, :], ident_bf16[:])
+                        for t in range(PACK):
+                            stats = work.tile([P, 6], F32, bufs=8)
+                            nc.vector.bn_stats(out=stats[:], in_=x_t[:, j - h, t, :])
+                            nc.vector.bn_aggr(out=mean_var[:, j * PACK + t, :], in_=stats[:])
+
+                std = work.tile([P, GROUP * PACK], F32)
+                nc.scalar.activation(out=std[:, :cols], in_=mean_var[:, :cols, 1], func=ACT.Sqrt, bias=BN_EPS)
+                rstd = work.tile([P, GROUP * PACK], F32)
+                nc.vector.reciprocal(out=rstd[:, :cols], in_=std[:, :cols])
+                gain = work.tile([P, GROUP * PACK], F32)
+                nc.vector.tensor_tensor(
+                    out=gain[:, :cols],
+                    in0=gamma_sb[:, n0 : n0 + gn, :].rearrange("p n t -> p (n t)"),
+                    in1=rstd[:, :cols],
+                    op=ALU.mult,
+                )
+                mean_gain = work.tile([P, GROUP * PACK], F32)
+                nc.vector.tensor_tensor(
+                    out=mean_gain[:, :cols], in0=mean_var[:, :cols, 0], in1=gain[:, :cols], op=ALU.mult
+                )
+                shift = work.tile([P, GROUP * PACK], F32)
+                nc.vector.tensor_tensor(
+                    out=shift[:, :cols],
+                    in0=beta_sb[:, n0 : n0 + gn, :].rearrange("p n t -> p (n t)"),
+                    in1=mean_gain[:, :cols],
+                    op=ALU.subtract,
+                )
+
+                bn_t = work.tile([P, GROUP, PACK, SAMPLES], F32)
+                sums_t = psum.tile([P, GROUP, P], F32)
+                for j in range(gn):
+                    x_t = x_pairs[j // 2]
+                    for t in range(PACK):
+                        col = j * PACK + t
+                        nc.scalar.activation(
+                            out=bn_t[:, j, t, :],
+                            in_=x_t[:, j % 2, t, :],
+                            func=ACT.Identity,
+                            scale=gain[:, col : col + 1],
+                            bias=shift[:, col : col + 1],
+                        )
+                    squares = work.tile([P, PACK, SAMPLES], F32, bufs=3)
+                    nc.scalar.activation(out=squares[:], in_=bn_t[:, j], func=ACT.Square)
+                    for t in range(PACK):
+                        nc.tensor.matmul(
+                            out=sums_t[:, j, :],
+                            lhsT=squares[:, t, :],
+                            rhs=ident_f32[:],
+                            is_transpose=True,
+                            start=(t == 0),
+                            stop=(t == PACK - 1),
+                        )
+
+                sum_sq = work.tile([P, GROUP], F32)
+                nc.vector.tensor_reduce(out=sum_sq[:, :gn], in_=sums_t[:, :gn, :], axis=AXIS.X, op=ALU.add)
+                nc.vector.tensor_scalar_max(out=sum_sq[:, :gn], in0=sum_sq[:, :gn], scalar1=L2_EPS_SQUARED)
+                norm = work.tile([P, GROUP], F32)
+                nc.scalar.activation(out=norm[:, :gn], in_=sum_sq[:, :gn], func=ACT.Sqrt)
+                rnorm = work.tile([P, GROUP], F32)
+                nc.vector.reciprocal(out=rnorm[:, :gn], in_=norm[:, :gn])
+
+                rnorm_all = psum.tile([P, GROUP, SAMPLES], F32)
+                for j in range(gn):
+                    nc.tensor.transpose(rnorm_all[:, j, :], rnorm[:, j : j + 1].to_broadcast([P, P]), ident_f32[:])
+
+                grouped = work.tile([P, GROUP, SAMPLES, PACK], BF16, align_bytes=64)
+                nc.vector.tensor_tensor(
+                    out=grouped[:, :gn],
+                    in0=bn_t[:, :gn].rearrange("p n t b -> p n b t"),
+                    in1=rnorm_all[:, :gn, :].unsqueeze(3).to_broadcast([P, gn, SAMPLES, PACK]),
+                    op=ALU.mult,
+                )
+                for j in range(gn):
+                    nc.vector.quantize_mx(
+                        out=emb_codes[:, n0 + j, :].bitcast(FP8X4),
+                        scales=emb_scales[:, n0 + j, :],
+                        in_=grouped[:, j].rearrange("p b t -> p (b t)"),
+                    )
+
+        with tc.tile_pool(name="fc_work", bufs=3, reuse_waits="tile") as work, tc.psum_pool(
+            name="fc_psum", bufs=2, reuse_waits="tile"
+        ) as psum:
+            for n in range(BINS):
+                sum_sq = work.tile([P, CHUNKS], F32, bufs=4)
+                for c in range(CHUNKS):
+                    fc_t = psum.tile([P, PACK, P], BF16, bufs=4)
+                    for t in range(PACK):
+                        nc.tensor.transpose(fc_t[:, t, :], fc_sb[:, n, t, c * P : (c + 1) * P], ident_bf16[:])
+                    unused = work.tile([P, PACK, P], BF16, bufs=4)
+                    nc.scalar.activation(
+                        out=unused[:], in_=fc_t[:], func=ACT.Square, accum_out=sum_sq[:, c : c + 1]
+                    )
+                nc.vector.tensor_scalar_max(out=sum_sq[:], in0=sum_sq[:], scalar1=L2_EPS_SQUARED)
+                norm = work.tile([P, CHUNKS], F32, bufs=4)
+                nc.scalar.activation(out=norm[:], in_=sum_sq[:], func=ACT.Sqrt)
+                rnorm = work.tile([P, CHUNKS], F32, bufs=4)
+                nc.vector.reciprocal(out=rnorm[:], in_=norm[:])
+
+                rnorm_all = psum.tile([P, CLASSES], F32)
+                for c in range(CHUNKS):
+                    nc.tensor.transpose(
+                        rnorm_all[:, c * P : (c + 1) * P], rnorm[:, c : c + 1].to_broadcast([P, P]), ident_f32[:]
+                    )
+
+                grouped = work.tile([P, CLASSES, PACK], BF16, align_bytes=64)
+                nc.vector.tensor_tensor(
+                    out=grouped[:],
+                    in0=fc_sb[:, n].rearrange("p t k -> p k t"),
+                    in1=rnorm_all[:].unsqueeze(2).to_broadcast([P, CLASSES, PACK]),
+                    op=ALU.mult,
+                )
+                fc_codes = work.tile([P, CLASSES], U32, align_bytes=64)
+                fc_scales = work.tile([P, CLASSES], U8, align_bytes=64)
+                nc.vector.quantize_mx(
+                    out=fc_codes[:].bitcast(FP8X4),
+                    scales=fc_scales[:],
+                    in_=grouped[:].rearrange("p k t -> p (k t)"),
+                )
+
+                logits = psum.tile([P, CLASSES], F32)
+                nc.tensor.matmul_mx(
+                    out=logits[:],
+                    lhsT=emb_codes[:, n, :].bitcast(FP8X4),
+                    lhsT_scale=emb_scales[:, n, :],
+                    rhs=fc_codes[:].bitcast(FP8X4),
+                    rhs_scale=fc_scales[:],
+                    start=True,
+                    stop=True,
+                )
+                slot = n % STORE_BINS
+                if slot == 0:
+                    staged = work.tile([P, STORE_BINS, CLASSES], F32)
+                nc.scalar.copy(out=staged[:, slot, :], in_=logits[:])
+                if slot == STORE_BINS - 1 or n == BINS - 1:
+                    nc.sync.dma_start(out=out[:, n - slot : n + 1, :], in_=staged[:, : slot + 1, :])

@@ -14,41 +14,53 @@ AXIS = mybir.AxisListType
 
 P = 128
 PACK = 4
+PAIR = 2
 BINS = 31
 SAMPLES = 128
 FEATURES = P * PACK
 CLASSES = 512
-CHUNKS = CLASSES // P
+HALVES = CLASSES // (P * PAIR)
 BN_EPS = 1e-5
 L2_EPS_SQUARED = 1e-24
 GROUP = 4
-STORE_BINS = 4
+BETA_ROW = 32
+STORE_BINS = 2
 
 FLOPS = 2 * BINS * SAMPLES * FEATURES * CLASSES
 
 
 def tile_gmpahead_pb_kernel(tc, emb, gamma, beta, fc1d, out):
     nc = tc.nc
+    groups = [(n0, min(GROUP, BINS - n0)) for n0 in range(0, BINS, GROUP)]
+
     with ExitStack() as ctx:
         keep = ctx.enter_context(tc.tile_pool(name="keep", bufs=1))
 
-        ident_bf16 = keep.tile([P, P], BF16)
-        make_identity(nc, ident_bf16[:])
         ident_f32 = keep.tile([P, P], F32)
         make_identity(nc, ident_f32[:])
+        minus_half = keep.tile([P, GROUP], F32)
+        nc.gpsimd.memset(minus_half[:], -0.5)
 
-        gamma_sb = keep.tile([P, BINS, PACK], BF16)
-        nc.scalar.dma_start(out=gamma_sb[:], in_=gamma.rearrange("n (p t) -> p n t", t=PACK))
-        beta_sb = keep.tile([P, BINS, PACK], BF16)
-        nc.scalar.dma_start(out=beta_sb[:], in_=beta.rearrange("n (p t) -> p n t", t=PACK))
+        def reciprocal_norms(pool, sum_sq, count):
+            clamped = pool.tile([P, GROUP], F32, bufs=6)
+            nc.gpsimd.tensor_scalar_max(out=clamped[:, :count], in0=sum_sq, scalar1=L2_EPS_SQUARED)
+            rnorm = pool.tile([P, GROUP], F32, bufs=6)
+            nc.gpsimd.tensor_tensor(
+                out=rnorm[:, :count], in0=clamped[:, :count], in1=minus_half[:, :count], op=ALU.pow
+            )
+            return rnorm
 
         emb_codes = keep.tile([P, BINS, SAMPLES], U32, align_bytes=64)
         emb_scales = keep.tile([P, BINS, SAMPLES], U8, align_bytes=64)
+        gain_rows = keep.tile([P, FEATURES], BF16)
+        gamma_beta = keep.tile([P, P, PACK], F32)
         fc_sb = keep.tile([P, BINS, PACK, CLASSES], BF16)
-
-        groups = [(n0, min(GROUP, BINS - n0)) for n0 in range(0, BINS, GROUP)]
+        fc_words = fc_sb[:].bitcast(F32)
 
         with tc.tile_pool(name="emb_work", bufs=2) as work, tc.psum_pool(name="emb_psum", bufs=2) as psum:
+            nc.vector.memset(gain_rows[:], 0.0)
+            nc.sync.dma_start(out=gain_rows[0:BINS, :], in_=gamma)
+            nc.sync.dma_start(out=gain_rows[BETA_ROW : BETA_ROW + BINS, :], in_=beta)
             emb_sb = work.tile([P, BINS, FEATURES], BF16, bufs=1)
             for n0, gn in groups:
                 nc.sync.dma_start(
@@ -61,57 +73,85 @@ def tile_gmpahead_pb_kernel(tc, emb, gamma, beta, fc1d, out):
                     in_=fc1d[n0 : n0 + gn].rearrange("n (p t) k -> p n (t k)", t=PACK),
                 )
 
-            for n0, gn in groups:
-                cols = gn * PACK
-                x_pairs = []
-                mean_var = work.tile([P, GROUP * PACK, 2], F32)
-                for h in range(0, gn, 2):
-                    x_t = psum.tile([P, 2, PACK, SAMPLES], BF16, bufs=4)
-                    x_pairs.append(x_t)
-                    for j in range(h, min(h + 2, gn)):
-                        by_t = emb_sb[:, n0 + j, :].rearrange("b (p t) -> b t p", t=PACK)
-                        for t in range(PACK):
-                            nc.tensor.transpose(x_t[:, j - h, t, :], by_t[:, t, :], ident_bf16[:])
-                        for t in range(PACK):
-                            stats = work.tile([P, 6], F32, bufs=8)
-                            nc.vector.bn_stats(out=stats[:], in_=x_t[:, j - h, t, :])
-                            nc.vector.bn_aggr(out=mean_var[:, j * PACK + t, :], in_=stats[:])
+            def features_to_partitions(dst, rows):
+                by_u = rows.bitcast(F32).rearrange("r (p u) -> r u p", u=PAIR)
+                for u in range(PAIR):
+                    nc.tensor.transpose(dst[:, u, :], by_u[:, u, :], ident_f32[:])
 
+            gain_t = psum.tile([P, PAIR, PAIR, P], F32, tag="x_t", bufs=4)
+            features_to_partitions(gain_t[:, 0], gain_rows[:])
+            nc.vector.tensor_copy(
+                out=gamma_beta[:].rearrange("p r (u e) -> p r u e", e=PAIR),
+                in_=gain_t[:, 0].bitcast(BF16).rearrange("p u (r e) -> p r u e", e=PAIR),
+            )
+
+            x_tiles = {}
+            gains = {}
+            shifts = {}
+            bn_tiles = {}
+            rnorms = {}
+
+            def emb_stats(g):
+                n0, gn = groups[g]
+                stats = work.tile([P, GROUP * PAIR, PAIR, 3], F32)
+                for h in range(0, gn, 2):
+                    x_t = psum.tile([P, 2, PAIR, SAMPLES], F32, tag="x_t", bufs=4)
+                    x_tiles[(g, h // 2)] = x_t
+                    for j in range(h, min(h + 2, gn)):
+                        features_to_partitions(x_t[:, j - h], emb_sb[:, n0 + j, :])
+                        for u in range(PAIR):
+                            nc.vector.bn_stats(
+                                out=stats[:, j * PAIR + u].rearrange("p e s -> p (e s)"),
+                                in_=x_t[:, j - h, u, :].bitcast(BF16),
+                            )
+                return stats
+
+            def emb_gain_shift(g, stats):
+                n0, gn = groups[g]
+                cols = gn * PACK
+                by_feature = stats[:].rearrange("p a e s -> p (a e) s")
                 std = work.tile([P, GROUP * PACK], F32)
-                nc.scalar.activation(out=std[:, :cols], in_=mean_var[:, :cols, 1], func=ACT.Sqrt, bias=BN_EPS)
+                nc.scalar.activation(
+                    out=std[:, :cols], in_=by_feature[:, :cols, 2], func=ACT.Sqrt, scale=1.0 / SAMPLES, bias=BN_EPS
+                )
                 rstd = work.tile([P, GROUP * PACK], F32)
                 nc.vector.reciprocal(out=rstd[:, :cols], in_=std[:, :cols])
-                gain = work.tile([P, GROUP * PACK], F32)
+                gain = work.tile([P, GROUP * PACK], F32, bufs=3)
                 nc.vector.tensor_tensor(
                     out=gain[:, :cols],
-                    in0=gamma_sb[:, n0 : n0 + gn, :].rearrange("p n t -> p (n t)"),
+                    in0=gamma_beta[:, n0 : n0 + gn, :].rearrange("p n t -> p (n t)"),
                     in1=rstd[:, :cols],
                     op=ALU.mult,
                 )
                 mean_gain = work.tile([P, GROUP * PACK], F32)
                 nc.vector.tensor_tensor(
-                    out=mean_gain[:, :cols], in0=mean_var[:, :cols, 0], in1=gain[:, :cols], op=ALU.mult
+                    out=mean_gain[:, :cols], in0=by_feature[:, :cols, 1], in1=gain[:, :cols], op=ALU.mult
                 )
-                shift = work.tile([P, GROUP * PACK], F32)
+                shift = work.tile([P, GROUP * PACK], F32, bufs=3)
                 nc.vector.tensor_tensor(
                     out=shift[:, :cols],
-                    in0=beta_sb[:, n0 : n0 + gn, :].rearrange("p n t -> p (n t)"),
+                    in0=gamma_beta[:, BETA_ROW + n0 : BETA_ROW + n0 + gn, :].rearrange("p n t -> p (n t)"),
                     in1=mean_gain[:, :cols],
                     op=ALU.subtract,
                 )
+                gains[g] = gain
+                shifts[g] = shift
 
-                bn_t = work.tile([P, GROUP, PACK, SAMPLES], F32)
+            def emb_norms(g):
+                n0, gn = groups[g]
+                bn_t = work.tile([P, GROUP, PACK, SAMPLES], F32, bufs=3)
+                bn_tiles[g] = bn_t
                 sums_t = psum.tile([P, GROUP, P], F32)
                 for j in range(gn):
-                    x_t = x_pairs[j // 2]
+                    x_bf = x_tiles[(g, j // 2)][:, j % 2].bitcast(BF16).rearrange("p u (b e) -> p u b e", e=PAIR)
                     for t in range(PACK):
                         col = j * PACK + t
                         nc.scalar.activation(
                             out=bn_t[:, j, t, :],
-                            in_=x_t[:, j % 2, t, :],
+                            in_=x_bf[:, t // PAIR, :, t % PAIR],
                             func=ACT.Identity,
-                            scale=gain[:, col : col + 1],
-                            bias=shift[:, col : col + 1],
+                            scale=gains[g][:, col : col + 1],
+                            bias=shifts[g][:, col : col + 1],
                         )
                     squares = work.tile([P, PACK, SAMPLES], F32, bufs=3)
                     nc.scalar.activation(out=squares[:], in_=bn_t[:, j], func=ACT.Square)
@@ -124,23 +164,21 @@ def tile_gmpahead_pb_kernel(tc, emb, gamma, beta, fc1d, out):
                             start=(t == 0),
                             stop=(t == PACK - 1),
                         )
-
-                sum_sq = work.tile([P, GROUP], F32)
+                sum_sq = work.tile([P, GROUP], F32, bufs=3)
                 nc.vector.tensor_reduce(out=sum_sq[:, :gn], in_=sums_t[:, :gn, :], axis=AXIS.X, op=ALU.add)
-                nc.vector.tensor_scalar_max(out=sum_sq[:, :gn], in0=sum_sq[:, :gn], scalar1=L2_EPS_SQUARED)
-                norm = work.tile([P, GROUP], F32)
-                nc.scalar.activation(out=norm[:, :gn], in_=sum_sq[:, :gn], func=ACT.Sqrt)
-                rnorm = work.tile([P, GROUP], F32)
-                nc.vector.reciprocal(out=rnorm[:, :gn], in_=norm[:, :gn])
+                rnorms[g] = reciprocal_norms(work, sum_sq[:, :gn], gn)
 
+            def emb_quantise(g):
+                n0, gn = groups[g]
                 rnorm_all = psum.tile([P, GROUP, SAMPLES], F32)
                 for j in range(gn):
-                    nc.tensor.transpose(rnorm_all[:, j, :], rnorm[:, j : j + 1].to_broadcast([P, P]), ident_f32[:])
-
+                    nc.tensor.transpose(
+                        rnorm_all[:, j, :], rnorms[g][:, j : j + 1].to_broadcast([P, P]), ident_f32[:]
+                    )
                 grouped = work.tile([P, GROUP, SAMPLES, PACK], BF16, align_bytes=64)
                 nc.vector.tensor_tensor(
                     out=grouped[:, :gn],
-                    in0=bn_t[:, :gn].rearrange("p n t b -> p n b t"),
+                    in0=bn_tiles[g][:, :gn].rearrange("p n t b -> p n b t"),
                     in1=rnorm_all[:, :gn, :].unsqueeze(3).to_broadcast([P, gn, SAMPLES, PACK]),
                     op=ALU.mult,
                 )
@@ -151,38 +189,58 @@ def tile_gmpahead_pb_kernel(tc, emb, gamma, beta, fc1d, out):
                         in_=grouped[:, j].rearrange("p b t -> p (b t)"),
                     )
 
+            for step in range(len(groups) + 2):
+                if step < len(groups):
+                    emb_gain_shift(step, emb_stats(step))
+                if 0 <= step - 2:
+                    emb_quantise(step - 2)
+                if 0 <= step - 1 < len(groups):
+                    emb_norms(step - 1)
+
         with tc.tile_pool(name="fc_work", bufs=3, reuse_waits="tile") as work, tc.psum_pool(
             name="fc_psum", bufs=2, reuse_waits="tile"
         ) as psum:
-            for n in range(BINS):
-                sum_sq = work.tile([P, CHUNKS], F32, bufs=4)
-                for c in range(CHUNKS):
-                    fc_t = psum.tile([P, PACK, P], BF16, bufs=4)
+            rnorms = {}
+            rnorm_alls = {}
+            codes = {}
+            scales = {}
+            stores = {}
+
+            def fc_norms(n):
+                sum_sq = work.tile([P, HALVES * PAIR], F32, bufs=4)
+                for h in range(HALVES):
+                    fc_t = psum.tile([P, PACK, P], F32, bufs=4)
                     for t in range(PACK):
-                        nc.tensor.transpose(fc_t[:, t, :], fc_sb[:, n, t, c * P : (c + 1) * P], ident_bf16[:])
-                    unused = work.tile([P, PACK, P], BF16, bufs=4)
-                    nc.scalar.activation(
-                        out=unused[:], in_=fc_t[:], func=ACT.Square, accum_out=sum_sq[:, c : c + 1]
-                    )
-                nc.vector.tensor_scalar_max(out=sum_sq[:], in0=sum_sq[:], scalar1=L2_EPS_SQUARED)
-                norm = work.tile([P, CHUNKS], F32, bufs=4)
-                nc.scalar.activation(out=norm[:], in_=sum_sq[:], func=ACT.Sqrt)
-                rnorm = work.tile([P, CHUNKS], F32, bufs=4)
-                nc.vector.reciprocal(out=rnorm[:], in_=norm[:])
+                        nc.tensor.transpose(fc_t[:, t, :], fc_words[:, n, t, h * P : (h + 1) * P], ident_f32[:])
+                    by_class = fc_t[:].bitcast(BF16).rearrange("k t (p e) -> k t p e", e=PAIR)
+                    for e in range(PAIR):
+                        unused = work.tile([P, PACK, P], BF16, bufs=4)
+                        col = h * PAIR + e
+                        nc.scalar.activation(
+                            out=unused[:], in_=by_class[:, :, :, e], func=ACT.Square, accum_out=sum_sq[:, col : col + 1]
+                        )
+                rnorms[n] = reciprocal_norms(work, sum_sq[:], HALVES * PAIR)
 
-                rnorm_all = psum.tile([P, CLASSES], F32)
-                for c in range(CHUNKS):
-                    nc.tensor.transpose(
-                        rnorm_all[:, c * P : (c + 1) * P], rnorm[:, c : c + 1].to_broadcast([P, P]), ident_f32[:]
-                    )
+            def fc_broadcast(n):
+                rnorm_all = psum.tile([P, HALVES, PAIR, P], F32)
+                rnorm_alls[n] = rnorm_all
+                for h in range(HALVES):
+                    for e in range(PAIR):
+                        col = h * PAIR + e
+                        nc.tensor.transpose(
+                            rnorm_all[:, h, e, :], rnorms[n][:, col : col + 1].to_broadcast([P, P]), ident_f32[:]
+                        )
 
+            def fc_quantise(n):
                 grouped = work.tile([P, CLASSES, PACK], BF16, align_bytes=64)
-                nc.vector.tensor_tensor(
-                    out=grouped[:],
-                    in0=fc_sb[:, n].rearrange("p t k -> p k t"),
-                    in1=rnorm_all[:].unsqueeze(2).to_broadcast([P, CLASSES, PACK]),
-                    op=ALU.mult,
-                )
+                for h in range(HALVES):
+                    block = slice(h * P * PAIR, (h + 1) * P * PAIR)
+                    nc.vector.tensor_tensor(
+                        out=grouped[:, block, :].rearrange("p (k e) t -> p k e t", e=PAIR),
+                        in0=fc_sb[:, n, :, block].rearrange("p t (k e) -> p k e t", e=PAIR),
+                        in1=rnorm_alls[n][:, h].rearrange("p e k -> p k e").unsqueeze(3).to_broadcast([P, P, PAIR, PACK]),
+                        op=ALU.mult,
+                    )
                 fc_codes = work.tile([P, CLASSES], U32, align_bytes=64)
                 fc_scales = work.tile([P, CLASSES], U8, align_bytes=64)
                 nc.vector.quantize_mx(
@@ -190,20 +248,35 @@ def tile_gmpahead_pb_kernel(tc, emb, gamma, beta, fc1d, out):
                     scales=fc_scales[:],
                     in_=grouped[:].rearrange("p k t -> p (k t)"),
                 )
+                codes[n] = fc_codes
+                scales[n] = fc_scales
 
+            def fc_multiply(n):
                 logits = psum.tile([P, CLASSES], F32)
                 nc.tensor.matmul_mx(
                     out=logits[:],
                     lhsT=emb_codes[:, n, :].bitcast(FP8X4),
                     lhsT_scale=emb_scales[:, n, :],
-                    rhs=fc_codes[:].bitcast(FP8X4),
-                    rhs_scale=fc_scales[:],
+                    rhs=codes[n][:].bitcast(FP8X4),
+                    rhs_scale=scales[n][:],
                     start=True,
                     stop=True,
                 )
                 slot = n % STORE_BINS
                 if slot == 0:
                     staged = work.tile([P, STORE_BINS, CLASSES], F32)
+                    stores[n // STORE_BINS] = staged
+                staged = stores[n // STORE_BINS]
                 nc.scalar.copy(out=staged[:, slot, :], in_=logits[:])
                 if slot == STORE_BINS - 1 or n == BINS - 1:
                     nc.sync.dma_start(out=out[:, n - slot : n + 1, :], in_=staged[:, : slot + 1, :])
+
+            for n in range(-4, BINS):
+                if n + 4 < BINS:
+                    fc_norms(n + 4)
+                if 0 <= n + 2 < BINS:
+                    fc_broadcast(n + 2)
+                if 0 <= n + 1 < BINS:
+                    fc_quantise(n + 1)
+                if 0 <= n:
+                    fc_multiply(n)

@@ -25,6 +25,8 @@ L2_EPS_SQUARED = 1e-24
 GROUP = 4
 BETA_ROW = 32
 STORE_BINS = 2
+NORMS_AHEAD = 4
+EMB_AHEAD = 5
 
 FLOPS = 2 * BINS * SAMPLES * FEATURES * CLASSES
 
@@ -35,248 +37,249 @@ def tile_gmpahead_pb_kernel(tc, emb, gamma, beta, fc1d, out):
 
     with ExitStack() as ctx:
         keep = ctx.enter_context(tc.tile_pool(name="keep", bufs=1))
+        work = ctx.enter_context(tc.tile_pool(name="work", bufs=2))
+        psum = ctx.enter_context(tc.psum_pool(name="psum", bufs=1))
 
         ident_f32 = keep.tile([P, P], F32)
         make_identity(nc, ident_f32[:])
         minus_half = keep.tile([P, GROUP], F32)
         nc.gpsimd.memset(minus_half[:], -0.5)
 
-        def reciprocal_norms(pool, sum_sq, count):
-            clamped = pool.tile([P, GROUP], F32, bufs=6)
+        emb_codes = keep.tile([P, BINS, SAMPLES], U32, align_bytes=64)
+        emb_scales = keep.tile([P, BINS, SAMPLES], U8, align_bytes=64)
+        gain_rows = keep.tile([P, FEATURES], BF16)
+        gamma_beta = keep.tile([P, P, PACK], F32)
+        emb_sb = keep.tile([P, BINS, FEATURES], BF16)
+        fc_sb = keep.tile([P, BINS, PACK, CLASSES], BF16)
+        fc_words = fc_sb[:].bitcast(F32)
+
+        nc.vector.memset(gain_rows[:], 0.0)
+        nc.sync.dma_start(out=gain_rows[0:BINS, :], in_=gamma)
+        nc.sync.dma_start(out=gain_rows[BETA_ROW : BETA_ROW + BINS, :], in_=beta)
+        for n0, gn in groups:
+            nc.sync.dma_start(out=emb_sb[:, n0 : n0 + gn, :], in_=emb[n0 : n0 + gn].rearrange("n b o -> b n o"))
+            for m0 in range(n0, n0 + gn, 2):
+                mn = min(2, n0 + gn - m0)
+                nc.sync.dma_start(
+                    out=fc_sb[:, m0 : m0 + mn].rearrange("p n t k -> p n (t k)"),
+                    in_=fc1d[m0 : m0 + mn].rearrange("n (p t) k -> p n (t k)", t=PACK),
+                )
+
+        def reciprocal_norms(sum_sq, count):
+            clamped = work.tile([P, GROUP], F32, bufs=8)
             nc.gpsimd.tensor_scalar_max(out=clamped[:, :count], in0=sum_sq, scalar1=L2_EPS_SQUARED)
-            rnorm = pool.tile([P, GROUP], F32, bufs=6)
+            rnorm = work.tile([P, GROUP], F32, bufs=8)
             nc.gpsimd.tensor_tensor(
                 out=rnorm[:, :count], in0=clamped[:, :count], in1=minus_half[:, :count], op=ALU.pow
             )
             return rnorm
 
-        emb_codes = keep.tile([P, BINS, SAMPLES], U32, align_bytes=64)
-        emb_scales = keep.tile([P, BINS, SAMPLES], U8, align_bytes=64)
-        gain_rows = keep.tile([P, FEATURES], BF16)
-        gamma_beta = keep.tile([P, P, PACK], F32)
-        fc_sb = keep.tile([P, BINS, PACK, CLASSES], BF16)
-        fc_words = fc_sb[:].bitcast(F32)
+        def features_to_partitions(dst, rows):
+            by_u = rows.bitcast(F32).rearrange("r (p u) -> r u p", u=PAIR)
+            for u in range(PAIR):
+                nc.tensor.transpose(dst[:, u, :], by_u[:, u, :], ident_f32[:])
 
-        with tc.tile_pool(name="emb_work", bufs=2) as work, tc.psum_pool(name="emb_psum", bufs=2) as psum:
-            nc.vector.memset(gain_rows[:], 0.0)
-            nc.sync.dma_start(out=gain_rows[0:BINS, :], in_=gamma)
-            nc.sync.dma_start(out=gain_rows[BETA_ROW : BETA_ROW + BINS, :], in_=beta)
-            emb_sb = work.tile([P, BINS, FEATURES], BF16, bufs=1)
-            for n0, gn in groups:
-                nc.sync.dma_start(
-                    out=emb_sb[:, n0 : n0 + gn, :], in_=emb[n0 : n0 + gn].rearrange("n b o -> b n o")
-                )
-            for n0 in range(0, BINS, 2):
-                gn = min(2, BINS - n0)
-                nc.sync.dma_start(
-                    out=fc_sb[:, n0 : n0 + gn].rearrange("p n t k -> p n (t k)"),
-                    in_=fc1d[n0 : n0 + gn].rearrange("n (p t) k -> p n (t k)", t=PACK),
-                )
+        gain_t = psum.tile([P, PAIR, PAIR, P], F32, tag="x_t", bufs=2)
+        features_to_partitions(gain_t[:, 0], gain_rows[:])
+        nc.vector.tensor_copy(
+            out=gamma_beta[:].rearrange("p r (u e) -> p r u e", e=PAIR),
+            in_=gain_t[:, 0].bitcast(BF16).rearrange("p u (r e) -> p r u e", e=PAIR),
+        )
 
-            def features_to_partitions(dst, rows):
-                by_u = rows.bitcast(F32).rearrange("r (p u) -> r u p", u=PAIR)
-                for u in range(PAIR):
-                    nc.tensor.transpose(dst[:, u, :], by_u[:, u, :], ident_f32[:])
+        x_tiles = {}
+        gains = {}
+        shifts = {}
+        bn_tiles = {}
+        sums_tiles = {}
+        sample_rnorms = {}
 
-            gain_t = psum.tile([P, PAIR, PAIR, P], F32, tag="x_t", bufs=4)
-            features_to_partitions(gain_t[:, 0], gain_rows[:])
-            nc.vector.tensor_copy(
-                out=gamma_beta[:].rearrange("p r (u e) -> p r u e", e=PAIR),
-                in_=gain_t[:, 0].bitcast(BF16).rearrange("p u (r e) -> p r u e", e=PAIR),
+        def emb_statistics(g):
+            n0, gn = groups[g]
+            cols = gn * PACK
+            stats = work.tile([P, GROUP * PAIR, PAIR, 3], F32)
+            for h in range(0, gn, 2):
+                x_t = psum.tile([P, 2, PAIR, SAMPLES], F32, tag="x_t", bufs=2)
+                x_tiles[(g, h // 2)] = x_t
+                for j in range(h, min(h + 2, gn)):
+                    features_to_partitions(x_t[:, j - h], emb_sb[:, n0 + j, :])
+                    for u in range(PAIR):
+                        nc.vector.bn_stats(
+                            out=stats[:, j * PAIR + u].rearrange("p e s -> p (e s)"),
+                            in_=x_t[:, j - h, u, :].bitcast(BF16),
+                        )
+            by_feature = stats[:].rearrange("p a e s -> p (a e) s")
+            std = work.tile([P, GROUP * PACK], F32)
+            nc.scalar.activation(
+                out=std[:, :cols], in_=by_feature[:, :cols, 2], func=ACT.Sqrt, scale=1.0 / SAMPLES, bias=BN_EPS
             )
+            rstd = work.tile([P, GROUP * PACK], F32)
+            nc.vector.reciprocal(out=rstd[:, :cols], in_=std[:, :cols])
+            gain = work.tile([P, GROUP * PACK], F32)
+            nc.vector.tensor_tensor(
+                out=gain[:, :cols],
+                in0=gamma_beta[:, n0 : n0 + gn, :].rearrange("p n t -> p (n t)"),
+                in1=rstd[:, :cols],
+                op=ALU.mult,
+            )
+            mean_gain = work.tile([P, GROUP * PACK], F32)
+            nc.vector.tensor_tensor(
+                out=mean_gain[:, :cols], in0=by_feature[:, :cols, 1], in1=gain[:, :cols], op=ALU.mult
+            )
+            shift = work.tile([P, GROUP * PACK], F32)
+            nc.vector.tensor_tensor(
+                out=shift[:, :cols],
+                in0=gamma_beta[:, BETA_ROW + n0 : BETA_ROW + n0 + gn, :].rearrange("p n t -> p (n t)"),
+                in1=mean_gain[:, :cols],
+                op=ALU.subtract,
+            )
+            gains[g] = gain
+            shifts[g] = shift
 
-            x_tiles = {}
-            gains = {}
-            shifts = {}
-            bn_tiles = {}
-            rnorms = {}
-
-            def emb_stats(g):
-                n0, gn = groups[g]
-                stats = work.tile([P, GROUP * PAIR, PAIR, 3], F32)
-                for h in range(0, gn, 2):
-                    x_t = psum.tile([P, 2, PAIR, SAMPLES], F32, tag="x_t", bufs=4)
-                    x_tiles[(g, h // 2)] = x_t
-                    for j in range(h, min(h + 2, gn)):
-                        features_to_partitions(x_t[:, j - h], emb_sb[:, n0 + j, :])
-                        for u in range(PAIR):
-                            nc.vector.bn_stats(
-                                out=stats[:, j * PAIR + u].rearrange("p e s -> p (e s)"),
-                                in_=x_t[:, j - h, u, :].bitcast(BF16),
-                            )
-                return stats
-
-            def emb_gain_shift(g, stats):
-                n0, gn = groups[g]
-                cols = gn * PACK
-                by_feature = stats[:].rearrange("p a e s -> p (a e) s")
-                std = work.tile([P, GROUP * PACK], F32)
-                nc.scalar.activation(
-                    out=std[:, :cols], in_=by_feature[:, :cols, 2], func=ACT.Sqrt, scale=1.0 / SAMPLES, bias=BN_EPS
-                )
-                rstd = work.tile([P, GROUP * PACK], F32)
-                nc.vector.reciprocal(out=rstd[:, :cols], in_=std[:, :cols])
-                gain = work.tile([P, GROUP * PACK], F32, bufs=3)
-                nc.vector.tensor_tensor(
-                    out=gain[:, :cols],
-                    in0=gamma_beta[:, n0 : n0 + gn, :].rearrange("p n t -> p (n t)"),
-                    in1=rstd[:, :cols],
-                    op=ALU.mult,
-                )
-                mean_gain = work.tile([P, GROUP * PACK], F32)
-                nc.vector.tensor_tensor(
-                    out=mean_gain[:, :cols], in0=by_feature[:, :cols, 1], in1=gain[:, :cols], op=ALU.mult
-                )
-                shift = work.tile([P, GROUP * PACK], F32, bufs=3)
-                nc.vector.tensor_tensor(
-                    out=shift[:, :cols],
-                    in0=gamma_beta[:, BETA_ROW + n0 : BETA_ROW + n0 + gn, :].rearrange("p n t -> p (n t)"),
-                    in1=mean_gain[:, :cols],
-                    op=ALU.subtract,
-                )
-                gains[g] = gain
-                shifts[g] = shift
-
-            def emb_norms(g):
-                n0, gn = groups[g]
-                bn_t = work.tile([P, GROUP, PACK, SAMPLES], F32, bufs=3)
+        def emb_batch_norm(g, j):
+            if j == 0:
+                bn_t = work.tile([P, GROUP, PACK, SAMPLES], F32)
                 bn_tiles[g] = bn_t
-                sums_t = psum.tile([P, GROUP, P], F32)
-                for j in range(gn):
-                    x_bf = x_tiles[(g, j // 2)][:, j % 2].bitcast(BF16).rearrange("p u (b e) -> p u b e", e=PAIR)
-                    for t in range(PACK):
-                        col = j * PACK + t
-                        nc.scalar.activation(
-                            out=bn_t[:, j, t, :],
-                            in_=x_bf[:, t // PAIR, :, t % PAIR],
-                            func=ACT.Identity,
-                            scale=gains[g][:, col : col + 1],
-                            bias=shifts[g][:, col : col + 1],
-                        )
-                    squares = work.tile([P, PACK, SAMPLES], F32, bufs=3)
-                    nc.scalar.activation(out=squares[:], in_=bn_t[:, j], func=ACT.Square)
-                    for t in range(PACK):
-                        nc.tensor.matmul(
-                            out=sums_t[:, j, :],
-                            lhsT=squares[:, t, :],
-                            rhs=ident_f32[:],
-                            is_transpose=True,
-                            start=(t == 0),
-                            stop=(t == PACK - 1),
-                        )
-                sum_sq = work.tile([P, GROUP], F32, bufs=3)
-                nc.vector.tensor_reduce(out=sum_sq[:, :gn], in_=sums_t[:, :gn, :], axis=AXIS.X, op=ALU.add)
-                rnorms[g] = reciprocal_norms(work, sum_sq[:, :gn], gn)
+                sums_t = psum.tile([P, GROUP, P], F32, tag="per_sample")
+                sums_tiles[g] = sums_t
+            bn_t = bn_tiles[g]
+            x_bf = x_tiles[(g, j // 2)][:, j % 2].bitcast(BF16).rearrange("p u (b e) -> p u b e", e=PAIR)
+            for t in range(PACK):
+                col = j * PACK + t
+                nc.scalar.activation(
+                    out=bn_t[:, j, t, :],
+                    in_=x_bf[:, t // PAIR, :, t % PAIR],
+                    func=ACT.Identity,
+                    scale=gains[g][:, col : col + 1],
+                    bias=shifts[g][:, col : col + 1],
+                )
+            squares = work.tile([P, PACK, SAMPLES], F32)
+            nc.scalar.activation(out=squares[:], in_=bn_t[:, j], func=ACT.Square)
+            for t in range(PACK):
+                nc.tensor.matmul(
+                    out=sums_tiles[g][:, j, :],
+                    lhsT=squares[:, t, :],
+                    rhs=ident_f32[:],
+                    is_transpose=True,
+                    start=(t == 0),
+                    stop=(t == PACK - 1),
+                )
 
-            def emb_quantise(g):
-                n0, gn = groups[g]
-                rnorm_all = psum.tile([P, GROUP, SAMPLES], F32)
-                for j in range(gn):
-                    nc.tensor.transpose(
-                        rnorm_all[:, j, :], rnorms[g][:, j : j + 1].to_broadcast([P, P]), ident_f32[:]
+        def emb_sample_norms(g):
+            n0, gn = groups[g]
+            sum_sq = work.tile([P, GROUP], F32, tag="sample_sum_sq")
+            nc.vector.tensor_reduce(out=sum_sq[:, :gn], in_=sums_tiles[g][:, :gn, :], axis=AXIS.X, op=ALU.add)
+            sample_rnorms[g] = reciprocal_norms(sum_sq[:, :gn], gn)
+
+        def emb_quantise(g):
+            n0, gn = groups[g]
+            rnorm_all = psum.tile([P, GROUP, SAMPLES], F32, tag="per_sample")
+            for j in range(gn):
+                nc.tensor.transpose(
+                    rnorm_all[:, j, :], sample_rnorms[g][:, j : j + 1].to_broadcast([P, P]), ident_f32[:]
+                )
+            grouped = work.tile([P, GROUP, SAMPLES, PACK], BF16, align_bytes=64, tag="emb_grouped", bufs=1)
+            nc.vector.tensor_tensor(
+                out=grouped[:, :gn],
+                in0=bn_tiles[g][:, :gn].rearrange("p n t b -> p n b t"),
+                in1=rnorm_all[:, :gn, :].unsqueeze(3).to_broadcast([P, gn, SAMPLES, PACK]),
+                op=ALU.mult,
+            )
+            for j in range(gn):
+                nc.vector.quantize_mx(
+                    out=emb_codes[:, n0 + j, :].bitcast(FP8X4),
+                    scales=emb_scales[:, n0 + j, :],
+                    in_=grouped[:, j].rearrange("p b t -> p (b t)"),
+                )
+
+        class_rnorms = {}
+        rnorm_alls = {}
+        codes = {}
+        scales = {}
+        stores = {}
+
+        def fc_norms(n):
+            sum_sq = work.tile([P, HALVES * PAIR], F32, tag="class_sum_sq", bufs=4)
+            for h in range(HALVES):
+                fc_t = psum.tile([P, PACK, P], F32, bufs=2)
+                for t in range(PACK):
+                    nc.tensor.transpose(fc_t[:, t, :], fc_words[:, n, t, h * P : (h + 1) * P], ident_f32[:])
+                by_class = fc_t[:].bitcast(BF16).rearrange("k t (p e) -> k t p e", e=PAIR)
+                for e in range(PAIR):
+                    unused = work.tile([P, PACK, P], BF16)
+                    col = h * PAIR + e
+                    nc.scalar.activation(
+                        out=unused[:], in_=by_class[:, :, :, e], func=ACT.Square, accum_out=sum_sq[:, col : col + 1]
                     )
-                grouped = work.tile([P, GROUP, SAMPLES, PACK], BF16, align_bytes=64)
+            class_rnorms[n] = reciprocal_norms(sum_sq[:], HALVES * PAIR)
+
+        def fc_broadcast(n):
+            rnorm_all = psum.tile([P, HALVES, PAIR, P], F32, tag="per_class", bufs=2)
+            rnorm_alls[n] = rnorm_all
+            for h in range(HALVES):
+                for e in range(PAIR):
+                    col = h * PAIR + e
+                    nc.tensor.transpose(
+                        rnorm_all[:, h, e, :], class_rnorms[n][:, col : col + 1].to_broadcast([P, P]), ident_f32[:]
+                    )
+
+        def fc_quantise(n):
+            grouped = work.tile([P, CLASSES, PACK], BF16, align_bytes=64, tag="fc_grouped")
+            for h in range(HALVES):
+                block = slice(h * P * PAIR, (h + 1) * P * PAIR)
                 nc.vector.tensor_tensor(
-                    out=grouped[:, :gn],
-                    in0=bn_tiles[g][:, :gn].rearrange("p n t b -> p n b t"),
-                    in1=rnorm_all[:, :gn, :].unsqueeze(3).to_broadcast([P, gn, SAMPLES, PACK]),
+                    out=grouped[:, block, :].rearrange("p (k e) t -> p k e t", e=PAIR),
+                    in0=fc_sb[:, n, :, block].rearrange("p t (k e) -> p k e t", e=PAIR),
+                    in1=rnorm_alls[n][:, h].rearrange("p e k -> p k e").unsqueeze(3).to_broadcast([P, P, PAIR, PACK]),
                     op=ALU.mult,
                 )
-                for j in range(gn):
-                    nc.vector.quantize_mx(
-                        out=emb_codes[:, n0 + j, :].bitcast(FP8X4),
-                        scales=emb_scales[:, n0 + j, :],
-                        in_=grouped[:, j].rearrange("p b t -> p (b t)"),
-                    )
+            fc_codes = work.tile([P, CLASSES], U32, align_bytes=64, bufs=3)
+            fc_scales = work.tile([P, CLASSES], U8, align_bytes=64, bufs=3)
+            nc.vector.quantize_mx(
+                out=fc_codes[:].bitcast(FP8X4),
+                scales=fc_scales[:],
+                in_=grouped[:].rearrange("p k t -> p (k t)"),
+            )
+            codes[n] = fc_codes
+            scales[n] = fc_scales
 
-            for step in range(len(groups) + 2):
-                if step < len(groups):
-                    emb_gain_shift(step, emb_stats(step))
-                if 0 <= step - 2:
-                    emb_quantise(step - 2)
-                if 0 <= step - 1 < len(groups):
-                    emb_norms(step - 1)
+        def fc_multiply(n):
+            logits = psum.tile([P, CLASSES], F32)
+            nc.tensor.matmul_mx(
+                out=logits[:],
+                lhsT=emb_codes[:, n, :].bitcast(FP8X4),
+                lhsT_scale=emb_scales[:, n, :],
+                rhs=codes[n][:].bitcast(FP8X4),
+                rhs_scale=scales[n][:],
+                start=True,
+                stop=True,
+            )
+            slot = n % STORE_BINS
+            if slot == 0:
+                staged = work.tile([P, STORE_BINS, CLASSES], F32)
+                stores[n // STORE_BINS] = staged
+            staged = stores[n // STORE_BINS]
+            nc.scalar.copy(out=staged[:, slot, :], in_=logits[:])
+            if slot == STORE_BINS - 1 or n == BINS - 1:
+                nc.sync.dma_start(out=out[:, n - slot : n + 1, :], in_=staged[:, : slot + 1, :])
 
-        with tc.tile_pool(name="fc_work", bufs=3, reuse_waits="tile") as work, tc.psum_pool(
-            name="fc_psum", bufs=2, reuse_waits="tile"
-        ) as psum:
-            rnorms = {}
-            rnorm_alls = {}
-            codes = {}
-            scales = {}
-            stores = {}
-
-            def fc_norms(n):
-                sum_sq = work.tile([P, HALVES * PAIR], F32, bufs=4)
-                for h in range(HALVES):
-                    fc_t = psum.tile([P, PACK, P], F32, bufs=4)
-                    for t in range(PACK):
-                        nc.tensor.transpose(fc_t[:, t, :], fc_words[:, n, t, h * P : (h + 1) * P], ident_f32[:])
-                    by_class = fc_t[:].bitcast(BF16).rearrange("k t (p e) -> k t p e", e=PAIR)
-                    for e in range(PAIR):
-                        unused = work.tile([P, PACK, P], BF16, bufs=4)
-                        col = h * PAIR + e
-                        nc.scalar.activation(
-                            out=unused[:], in_=by_class[:, :, :, e], func=ACT.Square, accum_out=sum_sq[:, col : col + 1]
-                        )
-                rnorms[n] = reciprocal_norms(work, sum_sq[:], HALVES * PAIR)
-
-            def fc_broadcast(n):
-                rnorm_all = psum.tile([P, HALVES, PAIR, P], F32)
-                rnorm_alls[n] = rnorm_all
-                for h in range(HALVES):
-                    for e in range(PAIR):
-                        col = h * PAIR + e
-                        nc.tensor.transpose(
-                            rnorm_all[:, h, e, :], rnorms[n][:, col : col + 1].to_broadcast([P, P]), ident_f32[:]
-                        )
-
-            def fc_quantise(n):
-                grouped = work.tile([P, CLASSES, PACK], BF16, align_bytes=64)
-                for h in range(HALVES):
-                    block = slice(h * P * PAIR, (h + 1) * P * PAIR)
-                    nc.vector.tensor_tensor(
-                        out=grouped[:, block, :].rearrange("p (k e) t -> p k e t", e=PAIR),
-                        in0=fc_sb[:, n, :, block].rearrange("p t (k e) -> p k e t", e=PAIR),
-                        in1=rnorm_alls[n][:, h].rearrange("p e k -> p k e").unsqueeze(3).to_broadcast([P, P, PAIR, PACK]),
-                        op=ALU.mult,
-                    )
-                fc_codes = work.tile([P, CLASSES], U32, align_bytes=64)
-                fc_scales = work.tile([P, CLASSES], U8, align_bytes=64)
-                nc.vector.quantize_mx(
-                    out=fc_codes[:].bitcast(FP8X4),
-                    scales=fc_scales[:],
-                    in_=grouped[:].rearrange("p k t -> p (k t)"),
-                )
-                codes[n] = fc_codes
-                scales[n] = fc_scales
-
-            def fc_multiply(n):
-                logits = psum.tile([P, CLASSES], F32)
-                nc.tensor.matmul_mx(
-                    out=logits[:],
-                    lhsT=emb_codes[:, n, :].bitcast(FP8X4),
-                    lhsT_scale=emb_scales[:, n, :],
-                    rhs=codes[n][:].bitcast(FP8X4),
-                    rhs_scale=scales[n][:],
-                    start=True,
-                    stop=True,
-                )
-                slot = n % STORE_BINS
-                if slot == 0:
-                    staged = work.tile([P, STORE_BINS, CLASSES], F32)
-                    stores[n // STORE_BINS] = staged
-                staged = stores[n // STORE_BINS]
-                nc.scalar.copy(out=staged[:, slot, :], in_=logits[:])
-                if slot == STORE_BINS - 1 or n == BINS - 1:
-                    nc.sync.dma_start(out=out[:, n - slot : n + 1, :], in_=staged[:, : slot + 1, :])
-
-            for n in range(-4, BINS):
-                if n + 4 < BINS:
-                    fc_norms(n + 4)
-                if 0 <= n + 2 < BINS:
-                    fc_broadcast(n + 2)
-                if 0 <= n + 1 < BINS:
-                    fc_quantise(n + 1)
-                if 0 <= n:
-                    fc_multiply(n)
+        for n in range(-EMB_AHEAD, BINS):
+            g, quarter = divmod(n + EMB_AHEAD, GROUP)
+            if g < len(groups):
+                gn = groups[g][1]
+                if quarter == 0:
+                    emb_statistics(g)
+                if quarter == 1 or quarter == 2:
+                    for j in range(2 * (quarter - 1), min(2 * quarter, gn)):
+                        emb_batch_norm(g, j)
+                if quarter == 2:
+                    emb_sample_norms(g)
+                if quarter == 3:
+                    emb_quantise(g)
+            if 0 <= n + NORMS_AHEAD < BINS:
+                fc_norms(n + NORMS_AHEAD)
+            if 0 <= n + 2 < BINS:
+                fc_broadcast(n + 2)
+            if 0 <= n + 1 < BINS:
+                fc_quantise(n + 1)
+            if 0 <= n:
+                fc_multiply(n)

@@ -26,7 +26,7 @@ GROUP = 4
 BETA_ROW = 32
 STORE_BINS = 2
 NORMS_AHEAD = 4
-EMB_AHEAD = 5
+EMB_AHEAD = 6
 
 FLOPS = 2 * BINS * SAMPLES * FEATURES * CLASSES
 
@@ -42,8 +42,6 @@ def tile_gmpahead_pb_kernel(tc, emb, gamma, beta, fc1d, out):
 
         ident_f32 = keep.tile([P, P], F32)
         make_identity(nc, ident_f32[:])
-        minus_half = keep.tile([P, GROUP], F32)
-        nc.gpsimd.memset(minus_half[:], -0.5)
 
         emb_codes = keep.tile([P, BINS, SAMPLES], U32, align_bytes=64)
         emb_scales = keep.tile([P, BINS, SAMPLES], U8, align_bytes=64)
@@ -66,12 +64,12 @@ def tile_gmpahead_pb_kernel(tc, emb, gamma, beta, fc1d, out):
                 )
 
         def reciprocal_norms(sum_sq, count):
-            clamped = work.tile([P, GROUP], F32, bufs=8)
-            nc.gpsimd.tensor_scalar_max(out=clamped[:, :count], in0=sum_sq, scalar1=L2_EPS_SQUARED)
+            excess = work.tile([P, GROUP], F32, bufs=8)
+            nc.scalar.activation(out=excess[:, :count], in_=sum_sq, func=ACT.Relu, bias=-L2_EPS_SQUARED)
+            norm = work.tile([P, GROUP], F32, bufs=8)
+            nc.scalar.activation(out=norm[:, :count], in_=excess[:, :count], func=ACT.Sqrt, bias=L2_EPS_SQUARED)
             rnorm = work.tile([P, GROUP], F32, bufs=8)
-            nc.gpsimd.tensor_tensor(
-                out=rnorm[:, :count], in0=clamped[:, :count], in1=minus_half[:, :count], op=ALU.pow
-            )
+            nc.vector.reciprocal(out=rnorm[:, :count], in_=norm[:, :count])
             return rnorm
 
         def features_to_partitions(dst, rows):
@@ -92,6 +90,7 @@ def tile_gmpahead_pb_kernel(tc, emb, gamma, beta, fc1d, out):
         bn_tiles = {}
         sums_tiles = {}
         sample_rnorms = {}
+        emb_grouped = {}
 
         def emb_statistics(g):
             n0, gn = groups[g]
@@ -115,18 +114,18 @@ def tile_gmpahead_pb_kernel(tc, emb, gamma, beta, fc1d, out):
             rstd = work.tile([P, GROUP * PACK], F32)
             nc.vector.reciprocal(out=rstd[:, :cols], in_=std[:, :cols])
             gain = work.tile([P, GROUP * PACK], F32)
-            nc.vector.tensor_tensor(
+            nc.gpsimd.tensor_tensor(
                 out=gain[:, :cols],
                 in0=gamma_beta[:, n0 : n0 + gn, :].rearrange("p n t -> p (n t)"),
                 in1=rstd[:, :cols],
                 op=ALU.mult,
             )
             mean_gain = work.tile([P, GROUP * PACK], F32)
-            nc.vector.tensor_tensor(
+            nc.gpsimd.tensor_tensor(
                 out=mean_gain[:, :cols], in0=by_feature[:, :cols, 1], in1=gain[:, :cols], op=ALU.mult
             )
             shift = work.tile([P, GROUP * PACK], F32)
-            nc.vector.tensor_tensor(
+            nc.gpsimd.tensor_tensor(
                 out=shift[:, :cols],
                 in0=gamma_beta[:, BETA_ROW + n0 : BETA_ROW + n0 + gn, :].rearrange("p n t -> p (n t)"),
                 in1=mean_gain[:, :cols],
@@ -153,7 +152,7 @@ def tile_gmpahead_pb_kernel(tc, emb, gamma, beta, fc1d, out):
                     bias=shifts[g][:, col : col + 1],
                 )
             squares = work.tile([P, PACK, SAMPLES], F32)
-            nc.scalar.activation(out=squares[:], in_=bn_t[:, j], func=ACT.Square)
+            nc.gpsimd.tensor_tensor(out=squares[:], in0=bn_t[:, j], in1=bn_t[:, j], op=ALU.mult)
             for t in range(PACK):
                 nc.tensor.matmul(
                     out=sums_tiles[g][:, j, :],
@@ -170,29 +169,36 @@ def tile_gmpahead_pb_kernel(tc, emb, gamma, beta, fc1d, out):
             nc.vector.tensor_reduce(out=sum_sq[:, :gn], in_=sums_tiles[g][:, :gn, :], axis=AXIS.X, op=ALU.add)
             sample_rnorms[g] = reciprocal_norms(sum_sq[:, :gn], gn)
 
-        def emb_quantise(g):
+        def emb_scale(g):
             n0, gn = groups[g]
             rnorm_all = psum.tile([P, GROUP, SAMPLES], F32, tag="per_sample")
             for j in range(gn):
                 nc.tensor.transpose(
                     rnorm_all[:, j, :], sample_rnorms[g][:, j : j + 1].to_broadcast([P, P]), ident_f32[:]
                 )
+            rnorm_sb = work.tile([P, GROUP, SAMPLES], F32, bufs=1)
+            nc.scalar.copy(out=rnorm_sb[:, :gn, :], in_=rnorm_all[:, :gn, :])
             grouped = work.tile([P, GROUP, SAMPLES, PACK], BF16, align_bytes=64, tag="emb_grouped", bufs=1)
-            nc.vector.tensor_tensor(
+            emb_grouped[g] = grouped
+            nc.gpsimd.tensor_tensor(
                 out=grouped[:, :gn],
                 in0=bn_tiles[g][:, :gn].rearrange("p n t b -> p n b t"),
-                in1=rnorm_all[:, :gn, :].unsqueeze(3).to_broadcast([P, gn, SAMPLES, PACK]),
+                in1=rnorm_sb[:, :gn, :].unsqueeze(3).to_broadcast([P, gn, SAMPLES, PACK]),
                 op=ALU.mult,
             )
+
+        def emb_quantise(g):
+            n0, gn = groups[g]
             for j in range(gn):
                 nc.vector.quantize_mx(
                     out=emb_codes[:, n0 + j, :].bitcast(FP8X4),
                     scales=emb_scales[:, n0 + j, :],
-                    in_=grouped[:, j].rearrange("p b t -> p (b t)"),
+                    in_=emb_grouped[g][:, j].rearrange("p b t -> p (b t)"),
                 )
 
         class_rnorms = {}
         rnorm_alls = {}
+        fc_grouped = {}
         codes = {}
         scales = {}
         stores = {}
@@ -222,8 +228,9 @@ def tile_gmpahead_pb_kernel(tc, emb, gamma, beta, fc1d, out):
                         rnorm_all[:, h, e, :], class_rnorms[n][:, col : col + 1].to_broadcast([P, P]), ident_f32[:]
                     )
 
-        def fc_quantise(n):
-            grouped = work.tile([P, CLASSES, PACK], BF16, align_bytes=64, tag="fc_grouped")
+        def fc_scale(n):
+            grouped = work.tile([P, CLASSES, PACK], BF16, align_bytes=64, tag="fc_grouped", bufs=3)
+            fc_grouped[n] = grouped
             for h in range(HALVES):
                 block = slice(h * P * PAIR, (h + 1) * P * PAIR)
                 nc.vector.tensor_tensor(
@@ -232,12 +239,14 @@ def tile_gmpahead_pb_kernel(tc, emb, gamma, beta, fc1d, out):
                     in1=rnorm_alls[n][:, h].rearrange("p e k -> p k e").unsqueeze(3).to_broadcast([P, P, PAIR, PACK]),
                     op=ALU.mult,
                 )
-            fc_codes = work.tile([P, CLASSES], U32, align_bytes=64, bufs=3)
-            fc_scales = work.tile([P, CLASSES], U8, align_bytes=64, bufs=3)
+
+        def fc_quantise(n):
+            fc_codes = work.tile([P, CLASSES], U32, align_bytes=64)
+            fc_scales = work.tile([P, CLASSES], U8, align_bytes=64)
             nc.vector.quantize_mx(
                 out=fc_codes[:].bitcast(FP8X4),
                 scales=fc_scales[:],
-                in_=grouped[:].rearrange("p k t -> p (k t)"),
+                in_=fc_grouped[n][:].rearrange("p k t -> p (k t)"),
             )
             codes[n] = fc_codes
             scales[n] = fc_scales
@@ -264,21 +273,24 @@ def tile_gmpahead_pb_kernel(tc, emb, gamma, beta, fc1d, out):
 
         for n in range(-EMB_AHEAD, BINS):
             g, quarter = divmod(n + EMB_AHEAD, GROUP)
-            if g < len(groups):
-                gn = groups[g][1]
-                if quarter == 0:
-                    emb_statistics(g)
-                if quarter == 1 or quarter == 2:
-                    for j in range(2 * (quarter - 1), min(2 * quarter, gn)):
-                        emb_batch_norm(g, j)
-                if quarter == 2:
-                    emb_sample_norms(g)
-                if quarter == 3:
-                    emb_quantise(g)
+            in_time = g < len(groups)
+            if in_time and quarter == 0:
+                emb_statistics(g)
+            if in_time and (quarter == 1 or quarter == 2):
+                for j in range(2 * (quarter - 1), min(2 * quarter, groups[g][1])):
+                    emb_batch_norm(g, j)
+            if in_time and quarter == 2:
+                emb_sample_norms(g)
+            if in_time and quarter == 3:
+                emb_scale(g)
             if 0 <= n + NORMS_AHEAD < BINS:
                 fc_norms(n + NORMS_AHEAD)
+            if 0 <= n + 3 < BINS:
+                fc_broadcast(n + 3)
             if 0 <= n + 2 < BINS:
-                fc_broadcast(n + 2)
+                fc_scale(n + 2)
+            if quarter == 0 and 1 <= g <= len(groups):
+                emb_quantise(g - 1)
             if 0 <= n + 1 < BINS:
                 fc_quantise(n + 1)
             if 0 <= n:

@@ -25,8 +25,8 @@ L2_EPS_SQUARED = 1e-24
 GROUP = 4
 BETA_ROW = 32
 STORE_BINS = 2
-NORMS_AHEAD = 4
-EMB_AHEAD = 6
+NORMS_AHEAD = 5
+EMB_AHEAD = 5
 
 FLOPS = 2 * BINS * SAMPLES * FEATURES * CLASSES
 
@@ -42,6 +42,8 @@ def tile_gmpahead_pb_kernel(tc, emb, gamma, beta, fc1d, out):
 
         ident_f32 = keep.tile([P, P], F32)
         make_identity(nc, ident_f32[:])
+        minus_half = keep.tile([P, GROUP], F32)
+        nc.gpsimd.memset(minus_half[:], -0.5)
 
         emb_codes = keep.tile([P, BINS, SAMPLES], U32, align_bytes=64)
         emb_scales = keep.tile([P, BINS, SAMPLES], U8, align_bytes=64)
@@ -54,22 +56,25 @@ def tile_gmpahead_pb_kernel(tc, emb, gamma, beta, fc1d, out):
         nc.vector.memset(gain_rows[:], 0.0)
         nc.sync.dma_start(out=gain_rows[0:BINS, :], in_=gamma)
         nc.sync.dma_start(out=gain_rows[BETA_ROW : BETA_ROW + BINS, :], in_=beta)
+        def fc_load(m0, mn):
+            nc.sync.dma_start(
+                out=fc_sb[:, m0 : m0 + mn].rearrange("p n t k -> p n (t k)"),
+                in_=fc1d[m0 : m0 + mn].rearrange("n (p t) k -> p n (t k)", t=PACK),
+            )
+
+        fc_load(0, 1)
         for n0, gn in groups:
             nc.sync.dma_start(out=emb_sb[:, n0 : n0 + gn, :], in_=emb[n0 : n0 + gn].rearrange("n b o -> b n o"))
-            for m0 in range(n0, n0 + gn, 2):
-                mn = min(2, n0 + gn - m0)
-                nc.sync.dma_start(
-                    out=fc_sb[:, m0 : m0 + mn].rearrange("p n t k -> p n (t k)"),
-                    in_=fc1d[m0 : m0 + mn].rearrange("n (p t) k -> p n (t k)", t=PACK),
-                )
+            for m0 in range(n0 + 1, min(n0 + GROUP + 1, BINS), 2):
+                fc_load(m0, min(2, BINS - m0))
 
         def reciprocal_norms(sum_sq, count):
-            excess = work.tile([P, GROUP], F32, bufs=8)
-            nc.scalar.activation(out=excess[:, :count], in_=sum_sq, func=ACT.Relu, bias=-L2_EPS_SQUARED)
-            norm = work.tile([P, GROUP], F32, bufs=8)
-            nc.scalar.activation(out=norm[:, :count], in_=excess[:, :count], func=ACT.Sqrt, bias=L2_EPS_SQUARED)
+            clamped = work.tile([P, GROUP], F32, bufs=8)
+            nc.gpsimd.tensor_scalar_max(out=clamped[:, :count], in0=sum_sq, scalar1=L2_EPS_SQUARED)
             rnorm = work.tile([P, GROUP], F32, bufs=8)
-            nc.vector.reciprocal(out=rnorm[:, :count], in_=norm[:, :count])
+            nc.gpsimd.tensor_tensor(
+                out=rnorm[:, :count], in0=clamped[:, :count], in1=minus_half[:, :count], op=ALU.pow
+            )
             return rnorm
 
         def features_to_partitions(dst, rows):
@@ -90,7 +95,6 @@ def tile_gmpahead_pb_kernel(tc, emb, gamma, beta, fc1d, out):
         bn_tiles = {}
         sums_tiles = {}
         sample_rnorms = {}
-        emb_grouped = {}
 
         def emb_statistics(g):
             n0, gn = groups[g]
@@ -114,18 +118,18 @@ def tile_gmpahead_pb_kernel(tc, emb, gamma, beta, fc1d, out):
             rstd = work.tile([P, GROUP * PACK], F32)
             nc.vector.reciprocal(out=rstd[:, :cols], in_=std[:, :cols])
             gain = work.tile([P, GROUP * PACK], F32)
-            nc.gpsimd.tensor_tensor(
+            nc.vector.tensor_tensor(
                 out=gain[:, :cols],
                 in0=gamma_beta[:, n0 : n0 + gn, :].rearrange("p n t -> p (n t)"),
                 in1=rstd[:, :cols],
                 op=ALU.mult,
             )
             mean_gain = work.tile([P, GROUP * PACK], F32)
-            nc.gpsimd.tensor_tensor(
+            nc.vector.tensor_tensor(
                 out=mean_gain[:, :cols], in0=by_feature[:, :cols, 1], in1=gain[:, :cols], op=ALU.mult
             )
             shift = work.tile([P, GROUP * PACK], F32)
-            nc.gpsimd.tensor_tensor(
+            nc.vector.tensor_tensor(
                 out=shift[:, :cols],
                 in0=gamma_beta[:, BETA_ROW + n0 : BETA_ROW + n0 + gn, :].rearrange("p n t -> p (n t)"),
                 in1=mean_gain[:, :cols],
@@ -152,7 +156,7 @@ def tile_gmpahead_pb_kernel(tc, emb, gamma, beta, fc1d, out):
                     bias=shifts[g][:, col : col + 1],
                 )
             squares = work.tile([P, PACK, SAMPLES], F32)
-            nc.gpsimd.tensor_tensor(out=squares[:], in0=bn_t[:, j], in1=bn_t[:, j], op=ALU.mult)
+            nc.scalar.activation(out=squares[:], in_=bn_t[:, j], func=ACT.Square)
             for t in range(PACK):
                 nc.tensor.matmul(
                     out=sums_tiles[g][:, j, :],
@@ -169,31 +173,25 @@ def tile_gmpahead_pb_kernel(tc, emb, gamma, beta, fc1d, out):
             nc.vector.tensor_reduce(out=sum_sq[:, :gn], in_=sums_tiles[g][:, :gn, :], axis=AXIS.X, op=ALU.add)
             sample_rnorms[g] = reciprocal_norms(sum_sq[:, :gn], gn)
 
-        def emb_scale(g):
+        def emb_quantise(g):
             n0, gn = groups[g]
             rnorm_all = psum.tile([P, GROUP, SAMPLES], F32, tag="per_sample")
             for j in range(gn):
                 nc.tensor.transpose(
                     rnorm_all[:, j, :], sample_rnorms[g][:, j : j + 1].to_broadcast([P, P]), ident_f32[:]
                 )
-            rnorm_sb = work.tile([P, GROUP, SAMPLES], F32, bufs=1)
-            nc.scalar.copy(out=rnorm_sb[:, :gn, :], in_=rnorm_all[:, :gn, :])
             grouped = work.tile([P, GROUP, SAMPLES, PACK], BF16, align_bytes=64, tag="emb_grouped", bufs=1)
-            emb_grouped[g] = grouped
-            nc.gpsimd.tensor_tensor(
+            nc.vector.tensor_tensor(
                 out=grouped[:, :gn],
                 in0=bn_tiles[g][:, :gn].rearrange("p n t b -> p n b t"),
-                in1=rnorm_sb[:, :gn, :].unsqueeze(3).to_broadcast([P, gn, SAMPLES, PACK]),
+                in1=rnorm_all[:, :gn, :].unsqueeze(3).to_broadcast([P, gn, SAMPLES, PACK]),
                 op=ALU.mult,
             )
-
-        def emb_quantise(g):
-            n0, gn = groups[g]
             for j in range(gn):
                 nc.vector.quantize_mx(
                     out=emb_codes[:, n0 + j, :].bitcast(FP8X4),
                     scales=emb_scales[:, n0 + j, :],
-                    in_=emb_grouped[g][:, j].rearrange("p b t -> p (b t)"),
+                    in_=grouped[:, j].rearrange("p b t -> p (b t)"),
                 )
 
         class_rnorms = {}
@@ -273,24 +271,23 @@ def tile_gmpahead_pb_kernel(tc, emb, gamma, beta, fc1d, out):
 
         for n in range(-EMB_AHEAD, BINS):
             g, quarter = divmod(n + EMB_AHEAD, GROUP)
-            in_time = g < len(groups)
-            if in_time and quarter == 0:
-                emb_statistics(g)
-            if in_time and (quarter == 1 or quarter == 2):
-                for j in range(2 * (quarter - 1), min(2 * quarter, groups[g][1])):
-                    emb_batch_norm(g, j)
-            if in_time and quarter == 2:
-                emb_sample_norms(g)
-            if in_time and quarter == 3:
-                emb_scale(g)
+            if g < len(groups):
+                gn = groups[g][1]
+                if quarter == 0:
+                    emb_statistics(g)
+                if quarter == 1 or quarter == 2:
+                    for j in range(2 * (quarter - 1), min(2 * quarter, gn)):
+                        emb_batch_norm(g, j)
+                if quarter == 2:
+                    emb_sample_norms(g)
+                if quarter == 3:
+                    emb_quantise(g)
             if 0 <= n + NORMS_AHEAD < BINS:
                 fc_norms(n + NORMS_AHEAD)
             if 0 <= n + 3 < BINS:
                 fc_broadcast(n + 3)
             if 0 <= n + 2 < BINS:
                 fc_scale(n + 2)
-            if quarter == 0 and 1 <= g <= len(groups):
-                emb_quantise(g - 1)
             if 0 <= n + 1 < BINS:
                 fc_quantise(n + 1)
             if 0 <= n:

@@ -24,6 +24,7 @@ BN_EPS = 1e-5
 L2_EPS_SQUARED = 1e-24
 GROUP = 4
 BETA_ROW = 32
+RUN = 4
 STORE_BINS = 2
 NORMS_AHEAD = 5
 EMB_AHEAD = 5
@@ -140,7 +141,7 @@ def tile_gmpahead_pb_kernel(tc, emb, gamma, beta, fc1d, out):
 
         def emb_batch_norm(g, j):
             if j == 0:
-                bn_t = work.tile([P, GROUP, PACK, SAMPLES], F32)
+                bn_t = work.tile([P, PACK, GROUP, SAMPLES], F32)
                 bn_tiles[g] = bn_t
                 sums_t = psum.tile([P, GROUP, P], F32, tag="per_sample")
                 sums_tiles[g] = sums_t
@@ -149,14 +150,14 @@ def tile_gmpahead_pb_kernel(tc, emb, gamma, beta, fc1d, out):
             for t in range(PACK):
                 col = j * PACK + t
                 nc.scalar.activation(
-                    out=bn_t[:, j, t, :],
+                    out=bn_t[:, t, j, :],
                     in_=x_bf[:, t // PAIR, :, t % PAIR],
                     func=ACT.Identity,
                     scale=gains[g][:, col : col + 1],
                     bias=shifts[g][:, col : col + 1],
                 )
             squares = work.tile([P, PACK, SAMPLES], F32)
-            nc.scalar.activation(out=squares[:], in_=bn_t[:, j], func=ACT.Square)
+            nc.scalar.activation(out=squares[:], in_=bn_t[:, :, j, :], func=ACT.Square)
             for t in range(PACK):
                 nc.tensor.matmul(
                     out=sums_tiles[g][:, j, :],
@@ -181,10 +182,11 @@ def tile_gmpahead_pb_kernel(tc, emb, gamma, beta, fc1d, out):
                     rnorm_all[:, j, :], sample_rnorms[g][:, j : j + 1].to_broadcast([P, P]), ident_f32[:]
                 )
             grouped = work.tile([P, GROUP, SAMPLES, PACK], BF16, align_bytes=64, tag="emb_grouped", bufs=1)
+            runs = gn * SAMPLES // RUN
             nc.vector.tensor_tensor(
-                out=grouped[:, :gn],
-                in0=bn_tiles[g][:, :gn].rearrange("p n t b -> p n b t"),
-                in1=rnorm_all[:, :gn, :].unsqueeze(3).to_broadcast([P, gn, SAMPLES, PACK]),
+                out=grouped[:, :gn].rearrange("p n (r i) t -> p (n r) t i", i=RUN),
+                in0=bn_tiles[g][:, :, :gn, :].rearrange("p t n (r i) -> p (n r) t i", i=RUN),
+                in1=rnorm_all[:, :gn, :].rearrange("p n (r i) -> p (n r) i", i=RUN).unsqueeze(2).to_broadcast([P, runs, PACK, RUN]),
                 op=ALU.mult,
             )
             for j in range(gn):
@@ -232,9 +234,9 @@ def tile_gmpahead_pb_kernel(tc, emb, gamma, beta, fc1d, out):
             for h in range(HALVES):
                 block = slice(h * P * PAIR, (h + 1) * P * PAIR)
                 nc.vector.tensor_tensor(
-                    out=grouped[:, block, :].rearrange("p (k e) t -> p k e t", e=PAIR),
-                    in0=fc_sb[:, n, :, block].rearrange("p t (k e) -> p k e t", e=PAIR),
-                    in1=rnorm_alls[n][:, h].rearrange("p e k -> p k e").unsqueeze(3).to_broadcast([P, P, PAIR, PACK]),
+                    out=grouped[:, block, :].rearrange("p (k e) t -> p k t e", e=PAIR),
+                    in0=fc_sb[:, n, :, block].rearrange("p t (k e) -> p k t e", e=PAIR),
+                    in1=rnorm_alls[n][:, h].rearrange("p e k -> p k e").unsqueeze(2).to_broadcast([P, P, PACK, PAIR]),
                     op=ALU.mult,
                 )
 

@@ -10,7 +10,6 @@ U32 = mybir.dt.uint32
 U8 = mybir.dt.uint8
 ALU = mybir.AluOpType
 ACT = mybir.ActivationFunctionType
-AXIS = mybir.AxisListType
 
 P = 128
 PACK = 4
@@ -20,206 +19,262 @@ SAMPLES = 128
 FEATURES = P * PACK
 CLASSES = 512
 HALVES = CLASSES // (P * PAIR)
+NORMS = HALVES * PAIR
 BN_EPS = 1e-5
 L2_EPS_SQUARED = 1e-24
-GROUP = 4
 BETA_ROW = 32
 RUN = 4
 STORE_BINS = 2
-NORMS_AHEAD = 5
-EMB_AHEAD = 5
+EMB_AHEAD = 9
+FC_AHEAD = 3
 
 FLOPS = 2 * BINS * SAMPLES * FEATURES * CLASSES
 
 
 def tile_gmpahead_pb_kernel(tc, emb, gamma, beta, fc1d, out):
     nc = tc.nc
-    groups = [(n0, min(GROUP, BINS - n0)) for n0 in range(0, BINS, GROUP)]
 
     with ExitStack() as ctx:
         keep = ctx.enter_context(tc.tile_pool(name="keep", bufs=1))
         work = ctx.enter_context(tc.tile_pool(name="work", bufs=2))
         psum = ctx.enter_context(tc.psum_pool(name="psum", bufs=1))
+        ctx.enter_context(tc.manual_schedule())
 
         ident_f32 = keep.tile([P, P], F32)
         make_identity(nc, ident_f32[:])
-        minus_half = keep.tile([P, GROUP], F32)
-        nc.gpsimd.memset(minus_half[:], -0.5)
+        ones = keep.tile([P, 1], F32)
+        nc.vector.memset(ones[:], 1.0)
 
-        emb_codes = keep.tile([P, BINS, SAMPLES], U32, align_bytes=64)
-        emb_scales = keep.tile([P, BINS, SAMPLES], U8, align_bytes=64)
         gain_rows = keep.tile([P, FEATURES], BF16)
         gamma_beta = keep.tile([P, P, PACK], F32)
         emb_sb = keep.tile([P, BINS, FEATURES], BF16)
         fc_sb = keep.tile([P, BINS, PACK, CLASSES], BF16)
         fc_words = fc_sb[:].bitcast(F32)
-
         nc.vector.memset(gain_rows[:], 0.0)
+
+        def emb_load(n0, n1):
+            nc.sync.dma_start(out=emb_sb[:, n0:n1, :], in_=emb[n0:n1].rearrange("n b o -> b n o"))
+
+        def fc_load(n):
+            nc.sync.dma_start(
+                out=fc_sb[:, n].rearrange("p t k -> p (t k)"), in_=fc1d[n].rearrange("(p t) k -> p (t k)", t=PACK)
+            )
+
+        emb_load(0, 2)
+        fc_load(0)
         nc.sync.dma_start(out=gain_rows[0:BINS, :], in_=gamma)
         nc.sync.dma_start(out=gain_rows[BETA_ROW : BETA_ROW + BINS, :], in_=beta)
-        def fc_load(m0, mn):
-            nc.sync.dma_start(
-                out=fc_sb[:, m0 : m0 + mn].rearrange("p n t k -> p n (t k)"),
-                in_=fc1d[m0 : m0 + mn].rearrange("n (p t) k -> p n (t k)", t=PACK),
-            )
-
-        fc_load(0, 1)
-        for n0, gn in groups:
-            nc.sync.dma_start(out=emb_sb[:, n0 : n0 + gn, :], in_=emb[n0 : n0 + gn].rearrange("n b o -> b n o"))
-            for m0 in range(n0 + 1, min(n0 + GROUP + 1, BINS), 2):
-                fc_load(m0, min(2, BINS - m0))
-
-        def reciprocal_norms(sum_sq, count):
-            clamped = work.tile([P, GROUP], F32, bufs=8)
-            nc.gpsimd.tensor_scalar_max(out=clamped[:, :count], in0=sum_sq, scalar1=L2_EPS_SQUARED)
-            rnorm = work.tile([P, GROUP], F32, bufs=8)
-            nc.gpsimd.tensor_tensor(
-                out=rnorm[:, :count], in0=clamped[:, :count], in1=minus_half[:, :count], op=ALU.pow
-            )
-            return rnorm
+        emb_load(2, 4)
+        fc_load(1)
+        emb_load(4, 8)
+        for n in range(2, BINS):
+            fc_load(n)
+            if n % 4 == 3 and n + 5 < BINS:
+                emb_load(n + 5, min(n + 9, BINS))
 
         def features_to_partitions(dst, rows):
             by_u = rows.bitcast(F32).rearrange("r (p u) -> r u p", u=PAIR)
             for u in range(PAIR):
                 nc.tensor.transpose(dst[:, u, :], by_u[:, u, :], ident_f32[:])
 
-        gain_t = psum.tile([P, PAIR, PAIR, P], F32, tag="x_t", bufs=2)
-        features_to_partitions(gain_t[:, 0], gain_rows[:])
-        nc.vector.tensor_copy(
-            out=gamma_beta[:].rearrange("p r (u e) -> p r u e", e=PAIR),
-            in_=gain_t[:, 0].bitcast(BF16).rearrange("p u (r e) -> p r u e", e=PAIR),
-        )
+        def load_gains():
+            gain_t = psum.tile([P, PAIR, PAIR, P], F32, tag="per_class")
+            features_to_partitions(gain_t[:, 0], gain_rows[:])
+            nc.vector.tensor_copy(
+                out=gamma_beta[:].rearrange("p r (u e) -> p r u e", e=PAIR),
+                in_=gain_t[:, 0].bitcast(BF16).rearrange("p u (r e) -> p r u e", e=PAIR),
+            )
 
         x_tiles = {}
+        stats_tiles = {}
+        rstds = {}
         gains = {}
         shifts = {}
         bn_tiles = {}
+        squares_tiles = {}
         sums_tiles = {}
         sample_rnorms = {}
+        rnorm_tiles = {}
+        grouped_tiles = {}
+        emb_codes = {}
+        emb_scales = {}
 
-        def emb_statistics(g):
-            n0, gn = groups[g]
-            cols = gn * PACK
-            stats = work.tile([P, GROUP * PAIR, PAIR, 3], F32)
-            for h in range(0, gn, 2):
-                x_t = psum.tile([P, 2, PAIR, SAMPLES], F32, tag="x_t", bufs=2)
-                x_tiles[(g, h // 2)] = x_t
-                for j in range(h, min(h + 2, gn)):
-                    features_to_partitions(x_t[:, j - h], emb_sb[:, n0 + j, :])
-                    for u in range(PAIR):
-                        nc.vector.bn_stats(
-                            out=stats[:, j * PAIR + u].rearrange("p e s -> p (e s)"),
-                            in_=x_t[:, j - h, u, :].bitcast(BF16),
-                        )
-            by_feature = stats[:].rearrange("p a e s -> p (a e) s")
-            std = work.tile([P, GROUP * PACK], F32)
+        def pair_bins(i):
+            return min(PAIR, BINS - PAIR * i)
+
+        def emb_statistics(n):
+            i, j = divmod(n, PAIR)
+            if j == 0:
+                x_t = psum.tile([P, PAIR, PAIR, SAMPLES], F32, bufs=2)
+                x_tiles[i] = x_t
+                stats = work.tile([P, PAIR, PAIR, PAIR, 3], F32, bufs=3)
+                stats_tiles[i] = stats
+                for k in range(pair_bins(i)):
+                    features_to_partitions(x_t[:, k], emb_sb[:, n + k, :])
+            for u in range(PAIR):
+                nc.vector.bn_stats(
+                    out=stats_tiles[i][:, j, u].rearrange("p e s -> p (e s)"),
+                    in_=x_tiles[i][:, j, u, :].bitcast(BF16),
+                )
+
+        def emb_rstd(i):
+            cols = pair_bins(i) * PACK
+            by_feature = stats_tiles[i][:].rearrange("p j u e s -> p (j u e) s")
+            rstd = work.tile([P, PAIR * PACK], F32)
             nc.scalar.activation(
-                out=std[:, :cols], in_=by_feature[:, :cols, 2], func=ACT.Sqrt, scale=1.0 / SAMPLES, bias=BN_EPS
+                out=rstd[:, :cols],
+                in_=by_feature[:, :cols, 2],
+                func=ACT.Abs_reciprocal_sqrt,
+                scale=1.0 / SAMPLES,
+                bias=BN_EPS,
             )
-            rstd = work.tile([P, GROUP * PACK], F32)
-            nc.vector.reciprocal(out=rstd[:, :cols], in_=std[:, :cols])
-            gain = work.tile([P, GROUP * PACK], F32)
-            nc.vector.tensor_tensor(
+            rstds[i] = rstd
+
+        def emb_gains(i):
+            n0, gn = PAIR * i, pair_bins(i)
+            cols = gn * PACK
+            means = stats_tiles[i][:].rearrange("p j u e s -> p (j u e) s")[:, :cols, 1]
+            gain = work.tile([P, PAIR * PACK], F32, bufs=3)
+            nc.gpsimd.tensor_tensor(
                 out=gain[:, :cols],
                 in0=gamma_beta[:, n0 : n0 + gn, :].rearrange("p n t -> p (n t)"),
-                in1=rstd[:, :cols],
+                in1=rstds[i][:, :cols],
                 op=ALU.mult,
             )
-            mean_gain = work.tile([P, GROUP * PACK], F32)
-            nc.vector.tensor_tensor(
-                out=mean_gain[:, :cols], in0=by_feature[:, :cols, 1], in1=gain[:, :cols], op=ALU.mult
-            )
-            shift = work.tile([P, GROUP * PACK], F32)
-            nc.vector.tensor_tensor(
+            mean_gain = work.tile([P, PAIR * PACK], F32)
+            nc.gpsimd.tensor_tensor(out=mean_gain[:, :cols], in0=means, in1=gain[:, :cols], op=ALU.mult)
+            shift = work.tile([P, PAIR * PACK], F32, bufs=3)
+            nc.gpsimd.tensor_tensor(
                 out=shift[:, :cols],
                 in0=gamma_beta[:, BETA_ROW + n0 : BETA_ROW + n0 + gn, :].rearrange("p n t -> p (n t)"),
                 in1=mean_gain[:, :cols],
                 op=ALU.subtract,
             )
-            gains[g] = gain
-            shifts[g] = shift
+            gains[i] = gain
+            shifts[i] = shift
 
-        def emb_batch_norm(g, j):
-            if j == 0:
-                bn_t = work.tile([P, PACK, GROUP, SAMPLES], F32)
-                bn_tiles[g] = bn_t
-                sums_t = psum.tile([P, GROUP, P], F32, tag="per_sample")
-                sums_tiles[g] = sums_t
-            bn_t = bn_tiles[g]
-            x_bf = x_tiles[(g, j // 2)][:, j % 2].bitcast(BF16).rearrange("p u (b e) -> p u b e", e=PAIR)
+        def emb_batch_norm(n):
+            i, j = divmod(n, PAIR)
+            bn_t = work.tile([P, PACK, SAMPLES], F32, bufs=5)
+            bn_tiles[n] = bn_t
+            x_bf = x_tiles[i][:, j].bitcast(BF16).rearrange("p u (b e) -> p u b e", e=PAIR)
             for t in range(PACK):
                 col = j * PACK + t
                 nc.scalar.activation(
-                    out=bn_t[:, t, j, :],
+                    out=bn_t[:, t, :],
                     in_=x_bf[:, t // PAIR, :, t % PAIR],
                     func=ACT.Identity,
-                    scale=gains[g][:, col : col + 1],
-                    bias=shifts[g][:, col : col + 1],
+                    scale=gains[i][:, col : col + 1],
+                    bias=shifts[i][:, col : col + 1],
                 )
-            squares = work.tile([P, PACK, SAMPLES], F32)
-            nc.scalar.activation(out=squares[:], in_=bn_t[:, :, j, :], func=ACT.Square)
+
+        def emb_squares(n):
+            squares = work.tile([P, PACK, SAMPLES], F32, bufs=3)
+            squares_tiles[n] = squares
+            nc.gpsimd.tensor_tensor(out=squares[:], in0=bn_tiles[n][:], in1=bn_tiles[n][:], op=ALU.mult)
+
+        def emb_sums(n):
+            i, j = divmod(n, PAIR)
+            if j == 0:
+                sums_t = psum.tile([P, PAIR], F32, tag="per_sample", bufs=2)
+                sums_tiles[i] = sums_t
             for t in range(PACK):
                 nc.tensor.matmul(
-                    out=sums_tiles[g][:, j, :],
-                    lhsT=squares[:, t, :],
-                    rhs=ident_f32[:],
-                    is_transpose=True,
+                    out=sums_tiles[i][:, j : j + 1],
+                    lhsT=squares_tiles[n][:, t, :],
+                    rhs=ones[:],
                     start=(t == 0),
                     stop=(t == PACK - 1),
                 )
 
-        def emb_sample_norms(g):
-            n0, gn = groups[g]
-            sum_sq = work.tile([P, GROUP], F32, tag="sample_sum_sq")
-            nc.vector.tensor_reduce(out=sum_sq[:, :gn], in_=sums_tiles[g][:, :gn, :], axis=AXIS.X, op=ALU.add)
-            sample_rnorms[g] = reciprocal_norms(sum_sq[:, :gn], gn)
+        def emb_sample_norms(i):
+            gn = pair_bins(i)
+            above = work.tile([P, PAIR], F32)
+            nc.scalar.activation(out=above[:, :gn], in_=sums_tiles[i][:, :gn], func=ACT.Relu, bias=-L2_EPS_SQUARED)
+            rnorm = work.tile([P, PAIR], F32, tag="sample_rnorm")
+            nc.scalar.activation(
+                out=rnorm[:, :gn], in_=above[:, :gn], func=ACT.Abs_reciprocal_sqrt, bias=L2_EPS_SQUARED
+            )
+            sample_rnorms[i] = rnorm
 
-        def emb_quantise(g):
-            n0, gn = groups[g]
-            rnorm_all = psum.tile([P, GROUP, SAMPLES], F32, tag="per_sample")
-            for j in range(gn):
+        def emb_broadcast(i):
+            rnorm_all = psum.tile([P, PAIR, SAMPLES], F32, tag="per_sample", bufs=2)
+            rnorm_tiles[i] = rnorm_all
+            for j in range(pair_bins(i)):
                 nc.tensor.transpose(
-                    rnorm_all[:, j, :], sample_rnorms[g][:, j : j + 1].to_broadcast([P, P]), ident_f32[:]
+                    rnorm_all[:, j, :], sample_rnorms[i][:, j : j + 1].to_broadcast([P, P]), ident_f32[:]
                 )
-            grouped = work.tile([P, GROUP, SAMPLES, PACK], BF16, align_bytes=64, tag="emb_grouped", bufs=1)
-            runs = gn * SAMPLES // RUN
+
+        def emb_scale(n):
+            i, j = divmod(n, PAIR)
+            if j == 0:
+                grouped = work.tile([P, PAIR, SAMPLES, PACK], BF16, align_bytes=64, tag="emb_grouped", bufs=2)
+                grouped_tiles[i] = grouped
+            runs = SAMPLES // RUN
             nc.vector.tensor_tensor(
-                out=grouped[:, :gn].rearrange("p n (r i) t -> p (n r) t i", i=RUN),
-                in0=bn_tiles[g][:, :, :gn, :].rearrange("p t n (r i) -> p (n r) t i", i=RUN),
-                in1=rnorm_all[:, :gn, :].rearrange("p n (r i) -> p (n r) i", i=RUN).unsqueeze(2).to_broadcast([P, runs, PACK, RUN]),
+                out=grouped_tiles[i][:, j].rearrange("p (r i) t -> p r t i", i=RUN),
+                in0=bn_tiles[n][:].rearrange("p t (r i) -> p r t i", i=RUN),
+                in1=rnorm_tiles[i][:, j].rearrange("p (r i) -> p r i", i=RUN).unsqueeze(2).to_broadcast([P, runs, PACK, RUN]),
                 op=ALU.mult,
             )
-            for j in range(gn):
-                nc.vector.quantize_mx(
-                    out=emb_codes[:, n0 + j, :].bitcast(FP8X4),
-                    scales=emb_scales[:, n0 + j, :],
-                    in_=grouped[:, j].rearrange("p b t -> p (b t)"),
-                )
 
+        def emb_quantise(i):
+            gn = pair_bins(i)
+            pair_codes = work.tile([P, PAIR, SAMPLES], U32, align_bytes=64, bufs=4)
+            pair_scales = work.tile([P, PAIR, SAMPLES], U8, align_bytes=64, bufs=4)
+            nc.vector.quantize_mx(
+                out=pair_codes[:, :gn].rearrange("p j b -> p (j b)").bitcast(FP8X4),
+                scales=pair_scales[:, :gn].rearrange("p j b -> p (j b)"),
+                in_=grouped_tiles[i][:, :gn].rearrange("p j b t -> p (j b t)"),
+            )
+            emb_codes[i] = pair_codes
+            emb_scales[i] = pair_scales
+
+        fc_transposed = {}
+        class_sums = {}
+        class_clamped = {}
         class_rnorms = {}
         rnorm_alls = {}
         fc_grouped = {}
         codes = {}
         scales = {}
+        logits_tiles = {}
         stores = {}
 
-        def fc_norms(n):
-            sum_sq = work.tile([P, HALVES * PAIR], F32, tag="class_sum_sq", bufs=4)
+        def fc_transpose(n):
             for h in range(HALVES):
                 fc_t = psum.tile([P, PACK, P], F32, bufs=2)
+                fc_transposed[(n, h)] = fc_t
                 for t in range(PACK):
                     nc.tensor.transpose(fc_t[:, t, :], fc_words[:, n, t, h * P : (h + 1) * P], ident_f32[:])
-                by_class = fc_t[:].bitcast(BF16).rearrange("k t (p e) -> k t p e", e=PAIR)
-                for e in range(PAIR):
-                    unused = work.tile([P, PACK, P], BF16)
-                    col = h * PAIR + e
-                    nc.scalar.activation(
-                        out=unused[:], in_=by_class[:, :, :, e], func=ACT.Square, accum_out=sum_sq[:, col : col + 1]
-                    )
-            class_rnorms[n] = reciprocal_norms(sum_sq[:], HALVES * PAIR)
+
+        def fc_squares(n, h):
+            if h == 0:
+                sum_sq = work.tile([P, NORMS], F32, tag="class_sum_sq", bufs=4)
+                class_sums[n] = sum_sq
+            by_class = fc_transposed[(n, h)][:].bitcast(BF16).rearrange("k t (p e) -> k t p e", e=PAIR)
+            for e in range(PAIR):
+                unused = work.tile([P, PACK, P], BF16)
+                col = h * PAIR + e
+                nc.scalar.activation(
+                    out=unused[:],
+                    in_=by_class[:, :, :, e],
+                    func=ACT.Square,
+                    accum_out=class_sums[n][:, col : col + 1],
+                )
+
+        def fc_clamp(n):
+            clamped = work.tile([P, NORMS], F32, tag="class_clamped", bufs=4)
+            nc.gpsimd.tensor_scalar_max(out=clamped[:], in0=class_sums[n][:], scalar1=L2_EPS_SQUARED)
+            class_clamped[n] = clamped
+
+        def fc_rnorm(n):
+            rnorm = work.tile([P, NORMS], F32, tag="class_rnorm", bufs=4)
+            nc.scalar.activation(out=rnorm[:], in_=class_clamped[n][:], func=ACT.Abs_reciprocal_sqrt)
+            class_rnorms[n] = rnorm
 
         def fc_broadcast(n):
-            rnorm_all = psum.tile([P, HALVES, PAIR, P], F32, tag="per_class", bufs=2)
+            rnorm_all = psum.tile([P, HALVES, PAIR, P], F32, tag="per_class")
             rnorm_alls[n] = rnorm_all
             for h in range(HALVES):
                 for e in range(PAIR):
@@ -241,8 +296,8 @@ def tile_gmpahead_pb_kernel(tc, emb, gamma, beta, fc1d, out):
                 )
 
         def fc_quantise(n):
-            fc_codes = work.tile([P, CLASSES], U32, align_bytes=64)
-            fc_scales = work.tile([P, CLASSES], U8, align_bytes=64)
+            fc_codes = work.tile([P, CLASSES], U32, align_bytes=64, bufs=4)
+            fc_scales = work.tile([P, CLASSES], U8, align_bytes=64, bufs=4)
             nc.vector.quantize_mx(
                 out=fc_codes[:].bitcast(FP8X4),
                 scales=fc_scales[:],
@@ -251,46 +306,91 @@ def tile_gmpahead_pb_kernel(tc, emb, gamma, beta, fc1d, out):
             codes[n] = fc_codes
             scales[n] = fc_scales
 
-        def fc_multiply(n):
+        def multiply(n):
+            i, j = divmod(n, PAIR)
             logits = psum.tile([P, CLASSES], F32)
+            logits_tiles[n] = logits
             nc.tensor.matmul_mx(
                 out=logits[:],
-                lhsT=emb_codes[:, n, :].bitcast(FP8X4),
-                lhsT_scale=emb_scales[:, n, :],
+                lhsT=emb_codes[i][:, j, :].bitcast(FP8X4),
+                lhsT_scale=emb_scales[i][:, j, :],
                 rhs=codes[n][:].bitcast(FP8X4),
                 rhs_scale=scales[n][:],
                 start=True,
                 stop=True,
             )
+
+        def copy_and_store(n):
             slot = n % STORE_BINS
             if slot == 0:
-                staged = work.tile([P, STORE_BINS, CLASSES], F32)
+                staged = work.tile([P, STORE_BINS, CLASSES], F32, bufs=5)
                 stores[n // STORE_BINS] = staged
             staged = stores[n // STORE_BINS]
-            nc.scalar.copy(out=staged[:, slot, :], in_=logits[:])
+            nc.scalar.copy(out=staged[:, slot, :], in_=logits_tiles[n][:])
             if slot == STORE_BINS - 1 or n == BINS - 1:
                 nc.sync.dma_start(out=out[:, n - slot : n + 1, :], in_=staged[:, : slot + 1, :])
 
-        for n in range(-EMB_AHEAD, BINS):
-            g, quarter = divmod(n + EMB_AHEAD, GROUP)
-            if g < len(groups):
-                gn = groups[g][1]
-                if quarter == 0:
-                    emb_statistics(g)
-                if quarter == 1 or quarter == 2:
-                    for j in range(2 * (quarter - 1), min(2 * quarter, gn)):
-                        emb_batch_norm(g, j)
-                if quarter == 2:
-                    emb_sample_norms(g)
-                if quarter == 3:
-                    emb_quantise(g)
-            if 0 <= n + NORMS_AHEAD < BINS:
-                fc_norms(n + NORMS_AHEAD)
-            if 0 <= n + 3 < BINS:
-                fc_broadcast(n + 3)
-            if 0 <= n + 2 < BINS:
-                fc_scale(n + 2)
-            if 0 <= n + 1 < BINS:
-                fc_quantise(n + 1)
-            if 0 <= n:
-                fc_multiply(n)
+        def for_pair(tick, phase, work_on_pair):
+            i, odd = divmod(tick - phase + EMB_AHEAD, PAIR)
+            if odd == 0 and 0 <= i and PAIR * i < BINS:
+                work_on_pair(i)
+
+        def for_bin(tick, phase, work_on_bin):
+            n = tick - phase + EMB_AHEAD
+            if 0 <= n < BINS:
+                work_on_bin(n)
+
+        def for_class_bin(n, work_on_bin):
+            if 0 <= n < BINS:
+                work_on_bin(n)
+
+        def tick_part(tick, part):
+            if part == 0:
+                for_pair(tick, 8, emb_quantise)
+                for_pair(tick, 5, emb_sample_norms)
+                for_bin(tick, 0, emb_statistics)
+                for_bin(tick, 6, emb_scale)
+            if part == 1:
+                for_bin(tick, 2, emb_batch_norm)
+                for_bin(tick, 2, emb_squares)
+                for_bin(tick, 3, emb_sums)
+            if part == 2:
+                for_pair(tick, 5, emb_broadcast)
+                for_pair(tick, 1, emb_rstd)
+                for_pair(tick, 1, emb_gains)
+
+        tick = -EMB_AHEAD
+        unstored = []
+        next_bin = 0
+        for step in range(-FC_AHEAD, BINS + 1):
+            for n in unstored:
+                copy_and_store(n)
+            unstored = []
+            for_class_bin(step + 1, fc_quantise)
+            for_class_bin(step + 2, fc_rnorm)
+            for catch_up in range(min(1, step - tick)):
+                for part in range(3):
+                    tick_part(tick, part)
+                tick += 1
+            tick_part(tick, 0)
+            for_class_bin(step + 3, fc_transpose)
+            if step == -FC_AHEAD:
+                load_gains()
+            for_class_bin(step + 2, fc_broadcast)
+            tick_part(tick, 1)
+            while next_bin <= min(step + 0, BINS - 1) and next_bin in codes and next_bin // PAIR in emb_codes:
+                for n in unstored:
+                    copy_and_store(n)
+                multiply(next_bin)
+                unstored = [next_bin]
+                next_bin += 1
+            if step + 3 < BINS:
+                fc_squares(step + 3, 0)
+            tick_part(tick, 2)
+            if step + 3 < BINS:
+                fc_squares(step + 3, 1)
+                fc_clamp(step + 3)
+            tick += 1
+            for_class_bin(step + 2, fc_scale)
+        for n in unstored:
+            copy_and_store(n)

@@ -265,12 +265,12 @@ def tile_gmpahead_pb_kernel(tc, emb, gamma, beta, fc1d, out):
 
         def fc_clamp(n):
             clamped = work.tile([P, NORMS], F32, tag="class_clamped", bufs=4)
-            nc.gpsimd.tensor_scalar_max(out=clamped[:], in0=class_sums[n][:], scalar1=L2_EPS_SQUARED)
+            nc.scalar.activation(out=clamped[:], in_=class_sums[n][:], func=ACT.Relu, bias=-L2_EPS_SQUARED)
             class_clamped[n] = clamped
 
         def fc_rnorm(n):
             rnorm = work.tile([P, NORMS], F32, tag="class_rnorm", bufs=4)
-            nc.scalar.activation(out=rnorm[:], in_=class_clamped[n][:], func=ACT.Abs_reciprocal_sqrt)
+            nc.scalar.activation(out=rnorm[:], in_=class_clamped[n][:], func=ACT.Abs_reciprocal_sqrt, bias=L2_EPS_SQUARED)
             class_rnorms[n] = rnorm
 
         def fc_broadcast(n):
@@ -367,6 +367,7 @@ def tile_gmpahead_pb_kernel(tc, emb, gamma, beta, fc1d, out):
                 copy_and_store(n)
             unstored = []
             for_class_bin(step + 1, fc_quantise)
+            for_class_bin(step + 2, fc_clamp)
             for_class_bin(step + 2, fc_rnorm)
             for catch_up in range(min(1, step - tick)):
                 for part in range(3):
@@ -389,7 +390,6 @@ def tile_gmpahead_pb_kernel(tc, emb, gamma, beta, fc1d, out):
             tick_part(tick, 2)
             if step + 3 < BINS:
                 fc_squares(step + 3, 1)
-                fc_clamp(step + 3)
             tick += 1
             for_class_bin(step + 2, fc_scale)
         for n in unstored:

@@ -93,6 +93,7 @@ def tile_gmpahead_pb_kernel(tc, emb, gamma, beta, fc1d, out):
         bn_tiles = {}
         squares_tiles = {}
         sums_tiles = {}
+        above_tiles = {}
         sample_rnorms = {}
         rnorm_tiles = {}
         grouped_tiles = {}
@@ -187,10 +188,15 @@ def tile_gmpahead_pb_kernel(tc, emb, gamma, beta, fc1d, out):
                     stop=(t == PACK - 1),
                 )
 
-        def emb_sample_norms(i):
+        def emb_norm_clamp(i):
             gn = pair_bins(i)
             above = work.tile([P, PAIR], F32)
             nc.scalar.activation(out=above[:, :gn], in_=sums_tiles[i][:, :gn], func=ACT.Relu, bias=-L2_EPS_SQUARED)
+            above_tiles[i] = above
+
+        def emb_sample_norms(i):
+            gn = pair_bins(i)
+            above = above_tiles[i]
             rnorm = work.tile([P, PAIR], F32, tag="sample_rnorm")
             nc.scalar.activation(
                 out=rnorm[:, :gn], in_=above[:, :gn], func=ACT.Abs_reciprocal_sqrt, bias=L2_EPS_SQUARED
@@ -346,15 +352,17 @@ def tile_gmpahead_pb_kernel(tc, emb, gamma, beta, fc1d, out):
 
         def tick_part(tick, part):
             if part == 0:
+                for_bin(tick, 0, emb_statistics)
+                for_pair(tick, 5, emb_norm_clamp)
+            if part == 1:
                 for_pair(tick, 8, emb_quantise)
                 for_pair(tick, 5, emb_sample_norms)
-                for_bin(tick, 0, emb_statistics)
                 for_bin(tick, 6, emb_scale)
-            if part == 1:
+            if part == 2:
                 for_bin(tick, 2, emb_batch_norm)
                 for_bin(tick, 2, emb_squares)
                 for_bin(tick, 3, emb_sums)
-            if part == 2:
+            if part == 3:
                 for_pair(tick, 5, emb_broadcast)
                 for_pair(tick, 1, emb_rstd)
                 for_pair(tick, 1, emb_gains)
@@ -366,19 +374,20 @@ def tile_gmpahead_pb_kernel(tc, emb, gamma, beta, fc1d, out):
             for n in unstored:
                 copy_and_store(n)
             unstored = []
-            for_class_bin(step + 1, fc_quantise)
             for_class_bin(step + 2, fc_clamp)
-            for_class_bin(step + 2, fc_rnorm)
             for catch_up in range(min(1, step - tick)):
-                for part in range(3):
+                for part in range(4):
                     tick_part(tick, part)
                 tick += 1
             tick_part(tick, 0)
+            for_class_bin(step + 1, fc_quantise)
+            for_class_bin(step + 2, fc_rnorm)
+            tick_part(tick, 1)
             for_class_bin(step + 3, fc_transpose)
             if step == -FC_AHEAD:
                 load_gains()
             for_class_bin(step + 2, fc_broadcast)
-            tick_part(tick, 1)
+            tick_part(tick, 2)
             while next_bin <= min(step + 0, BINS - 1) and next_bin in codes and next_bin // PAIR in emb_codes:
                 for n in unstored:
                     copy_and_store(n)
@@ -387,7 +396,7 @@ def tile_gmpahead_pb_kernel(tc, emb, gamma, beta, fc1d, out):
                 next_bin += 1
             if step + 3 < BINS:
                 fc_squares(step + 3, 0)
-            tick_part(tick, 2)
+            tick_part(tick, 3)
             if step + 3 < BINS:
                 fc_squares(step + 3, 1)
             tick += 1

@@ -42,8 +42,6 @@ def tile_gmpahead_pb_kernel(tc, emb, gamma, beta, fc1d, out):
 
         ident_f32 = keep.tile([P, P], F32)
         make_identity(nc, ident_f32[:])
-        ones = keep.tile([P, 1], F32)
-        nc.vector.memset(ones[:], 1.0)
 
         gain_rows = keep.tile([P, FEATURES], BF16)
         gamma_beta = keep.tile([P, P, PACK], F32)
@@ -93,6 +91,7 @@ def tile_gmpahead_pb_kernel(tc, emb, gamma, beta, fc1d, out):
         bn_tiles = {}
         squares_tiles = {}
         sums_tiles = {}
+        sample_sums = {}
         above_tiles = {}
         sample_rnorms = {}
         rnorm_tiles = {}
@@ -156,7 +155,7 @@ def tile_gmpahead_pb_kernel(tc, emb, gamma, beta, fc1d, out):
 
         def emb_batch_norm(n):
             i, j = divmod(n, PAIR)
-            bn_t = work.tile([P, PACK, SAMPLES], F32, bufs=5)
+            bn_t = work.tile([P, PACK, SAMPLES], F32, bufs=7)
             bn_tiles[n] = bn_t
             x_bf = x_tiles[i][:, j].bitcast(BF16).rearrange("p u (b e) -> p u b e", e=PAIR)
             for t in range(PACK):
@@ -177,21 +176,32 @@ def tile_gmpahead_pb_kernel(tc, emb, gamma, beta, fc1d, out):
         def emb_sums(n):
             i, j = divmod(n, PAIR)
             if j == 0:
-                sums_t = psum.tile([P, PAIR], F32, tag="per_sample", bufs=2)
+                sums_t = psum.tile([P, PAIR, P], F32, tag="per_sample", bufs=2)
                 sums_tiles[i] = sums_t
             for t in range(PACK):
                 nc.tensor.matmul(
-                    out=sums_tiles[i][:, j : j + 1],
+                    out=sums_tiles[i][:, j, :],
                     lhsT=squares_tiles[n][:, t, :],
-                    rhs=ones[:],
+                    rhs=ident_f32[:],
+                    is_transpose=True,
                     start=(t == 0),
                     stop=(t == PACK - 1),
                 )
 
+        def emb_finish_sums(n):
+            i, j = divmod(n, PAIR)
+            if j == 0:
+                sum_sq = work.tile([P, PAIR], F32, tag="sample_sum_sq", bufs=3)
+                sample_sums[i] = sum_sq
+            unused = work.tile([P, P], F32, tag="unused_sums")
+            nc.scalar.activation(
+                out=unused[:], in_=sums_tiles[i][:, j, :], func=ACT.Identity, accum_out=sample_sums[i][:, j : j + 1]
+            )
+
         def emb_norm_clamp(i):
             gn = pair_bins(i)
             above = work.tile([P, PAIR], F32)
-            nc.scalar.activation(out=above[:, :gn], in_=sums_tiles[i][:, :gn], func=ACT.Relu, bias=-L2_EPS_SQUARED)
+            nc.scalar.activation(out=above[:, :gn], in_=sample_sums[i][:, :gn], func=ACT.Relu, bias=-L2_EPS_SQUARED)
             above_tiles[i] = above
 
         def emb_sample_norms(i):
@@ -353,6 +363,7 @@ def tile_gmpahead_pb_kernel(tc, emb, gamma, beta, fc1d, out):
         def tick_part(tick, part):
             if part == 0:
                 for_bin(tick, 0, emb_statistics)
+                for_bin(tick, 4, emb_finish_sums)
                 for_pair(tick, 5, emb_norm_clamp)
             if part == 1:
                 for_pair(tick, 8, emb_quantise)

@@ -27,6 +27,8 @@ RUN = 4
 STORE_BINS = 2
 EMB_AHEAD = 9
 FC_AHEAD = 3
+LAST = 2
+EMB_LAG = 1
 
 FLOPS = 2 * BINS * SAMPLES * FEATURES * CLASSES
 
@@ -95,9 +97,13 @@ def tile_gmpahead_pb_kernel(tc, emb, gamma, beta, fc1d, out):
         above_tiles = {}
         sample_rnorms = {}
         rnorm_tiles = {}
+        rnorm_copies = {}
         grouped_tiles = {}
         emb_codes = {}
         emb_scales = {}
+
+        def on_gpsimd(n):
+            return True
 
         def pair_bins(i):
             return min(PAIR, BINS - PAIR * i)
@@ -155,18 +161,19 @@ def tile_gmpahead_pb_kernel(tc, emb, gamma, beta, fc1d, out):
 
         def emb_batch_norm(n):
             i, j = divmod(n, PAIR)
-            bn_t = work.tile([P, PACK, SAMPLES], F32, bufs=7)
+            bn_t = work.tile([P, PACK, SAMPLES], F32, bufs=8)
             bn_tiles[n] = bn_t
             x_bf = x_tiles[i][:, j].bitcast(BF16).rearrange("p u (b e) -> p u b e", e=PAIR)
             for t in range(PACK):
                 col = j * PACK + t
-                nc.scalar.activation(
-                    out=bn_t[:, t, :],
-                    in_=x_bf[:, t // PAIR, :, t % PAIR],
-                    func=ACT.Identity,
-                    scale=gains[i][:, col : col + 1],
-                    bias=shifts[i][:, col : col + 1],
-                )
+                x_col = x_bf[:, t // PAIR, :, t % PAIR]
+                gain, shift = gains[i][:, col : col + 1], shifts[i][:, col : col + 1]
+                if n % 2 == 1:
+                    nc.vector.tensor_scalar(
+                        out=bn_t[:, t, :], in0=x_col, scalar1=gain, scalar2=shift, op0=ALU.mult, op1=ALU.add
+                    )
+                else:
+                    nc.scalar.activation(out=bn_t[:, t, :], in_=x_col, func=ACT.Identity, scale=gain, bias=shift)
 
         def emb_squares(n):
             squares = work.tile([P, PACK, SAMPLES], F32, bufs=3)
@@ -221,16 +228,25 @@ def tile_gmpahead_pb_kernel(tc, emb, gamma, beta, fc1d, out):
                     rnorm_all[:, j, :], sample_rnorms[i][:, j : j + 1].to_broadcast([P, P]), ident_f32[:]
                 )
 
+        def emb_rnorm_copy(n):
+            if on_gpsimd(n):
+                i, j = divmod(n, PAIR)
+                rnorm_sb = work.tile([P, SAMPLES], F32, bufs=2)
+                nc.scalar.copy(out=rnorm_sb[:], in_=rnorm_tiles[i][:, j, :])
+                rnorm_copies[n] = rnorm_sb
+
         def emb_scale(n):
             i, j = divmod(n, PAIR)
             if j == 0:
                 grouped = work.tile([P, PAIR, SAMPLES, PACK], BF16, align_bytes=64, tag="emb_grouped", bufs=2)
                 grouped_tiles[i] = grouped
             runs = SAMPLES // RUN
-            nc.vector.tensor_tensor(
+            engine = nc.gpsimd if on_gpsimd(n) else nc.vector
+            rnorm = rnorm_copies[n][:] if on_gpsimd(n) else rnorm_tiles[i][:, j]
+            engine.tensor_tensor(
                 out=grouped_tiles[i][:, j].rearrange("p (r i) t -> p r t i", i=RUN),
                 in0=bn_tiles[n][:].rearrange("p t (r i) -> p r t i", i=RUN),
-                in1=rnorm_tiles[i][:, j].rearrange("p (r i) -> p r i", i=RUN).unsqueeze(2).to_broadcast([P, runs, PACK, RUN]),
+                in1=rnorm.rearrange("p (r i) -> p r i", i=RUN).unsqueeze(2).to_broadcast([P, runs, PACK, RUN]),
                 op=ALU.mult,
             )
 
@@ -312,8 +328,8 @@ def tile_gmpahead_pb_kernel(tc, emb, gamma, beta, fc1d, out):
                 )
 
         def fc_quantise(n):
-            fc_codes = work.tile([P, CLASSES], U32, align_bytes=64, bufs=4)
-            fc_scales = work.tile([P, CLASSES], U8, align_bytes=64, bufs=4)
+            fc_codes = work.tile([P, CLASSES], U32, align_bytes=64, bufs=5)
+            fc_scales = work.tile([P, CLASSES], U8, align_bytes=64, bufs=5)
             nc.vector.quantize_mx(
                 out=fc_codes[:].bitcast(FP8X4),
                 scales=fc_scales[:],
@@ -324,7 +340,10 @@ def tile_gmpahead_pb_kernel(tc, emb, gamma, beta, fc1d, out):
 
         def multiply(n):
             i, j = divmod(n, PAIR)
-            logits = psum.tile([P, CLASSES], F32)
+            if n >= BINS - LAST:
+                logits = psum.tile([P, CLASSES], F32, tag="x_t", bufs=2)
+            else:
+                logits = psum.tile([P, CLASSES], F32)
             logits_tiles[n] = logits
             nc.tensor.matmul_mx(
                 out=logits[:],
@@ -339,10 +358,13 @@ def tile_gmpahead_pb_kernel(tc, emb, gamma, beta, fc1d, out):
         def copy_and_store(n):
             slot = n % STORE_BINS
             if slot == 0:
-                staged = work.tile([P, STORE_BINS, CLASSES], F32, bufs=5)
+                staged = work.tile([P, STORE_BINS, CLASSES], F32, bufs=3)
                 stores[n // STORE_BINS] = staged
             staged = stores[n // STORE_BINS]
-            nc.scalar.copy(out=staged[:, slot, :], in_=logits_tiles[n][:])
+            if n >= BINS - LAST and n % 2 == 1:
+                nc.vector.tensor_copy(out=staged[:, slot, :], in_=logits_tiles[n][:])
+            else:
+                nc.scalar.copy(out=staged[:, slot, :], in_=logits_tiles[n][:])
             if slot == STORE_BINS - 1 or n == BINS - 1:
                 nc.sync.dma_start(out=out[:, n - slot : n + 1, :], in_=staged[:, : slot + 1, :])
 
@@ -368,25 +390,26 @@ def tile_gmpahead_pb_kernel(tc, emb, gamma, beta, fc1d, out):
             if part == 1:
                 for_pair(tick, 8, emb_quantise)
                 for_pair(tick, 5, emb_sample_norms)
+                for_bin(tick, 6, emb_rnorm_copy)
                 for_bin(tick, 6, emb_scale)
             if part == 2:
                 for_bin(tick, 2, emb_batch_norm)
-                for_bin(tick, 2, emb_squares)
-                for_bin(tick, 3, emb_sums)
-            if part == 3:
-                for_pair(tick, 5, emb_broadcast)
                 for_pair(tick, 1, emb_rstd)
                 for_pair(tick, 1, emb_gains)
+                for_bin(tick, 2, emb_squares)
+            if part == 3:
+                for_bin(tick, 3, emb_sums)
+                for_pair(tick, 5, emb_broadcast)
 
         tick = -EMB_AHEAD
         unstored = []
         next_bin = 0
-        for step in range(-FC_AHEAD, BINS + 1):
+        for step in range(-FC_AHEAD, BINS + 1 + EMB_LAG):
             for n in unstored:
                 copy_and_store(n)
             unstored = []
             for_class_bin(step + 2, fc_clamp)
-            for catch_up in range(min(1, step - tick)):
+            for catch_up in range(min(1, step - EMB_LAG - tick)):
                 for part in range(4):
                     tick_part(tick, part)
                 tick += 1
@@ -399,7 +422,7 @@ def tile_gmpahead_pb_kernel(tc, emb, gamma, beta, fc1d, out):
                 load_gains()
             for_class_bin(step + 2, fc_broadcast)
             tick_part(tick, 2)
-            while next_bin <= min(step + 0, BINS - 1) and next_bin in codes and next_bin // PAIR in emb_codes:
+            while next_bin <= min(step - EMB_LAG, BINS - 1) and next_bin in codes and next_bin // PAIR in emb_codes:
                 for n in unstored:
                     copy_and_store(n)
                 multiply(next_bin)

from contextlib import ExitStack

import concourse.mybir as mybir
from concourse.masks import make_identity

FP8X4 = mybir.dt.float8_e4m3fn_x4
BF16 = mybir.dt.bfloat16
F32 = mybir.dt.float32
U32 = mybir.dt.uint32
U8 = mybir.dt.uint8
ALU = mybir.AluOpType
ACT = mybir.ActivationFunctionType

P = 128
PACK = 4
PAIR = 2
BINS = 31
SAMPLES = 128
FEATURES = P * PACK
CLASSES = 512
HALVES = CLASSES // (P * PAIR)
NORMS = HALVES * PAIR
BN_EPS = 1e-5
L2_EPS_SQUARED = 1e-24
BETA_ROW = 32
RUN = 4
STORE_BINS = 2
EMB_AHEAD = 9
FC_AHEAD = 3
LAST = 2
EMB_LAG = 1

FLOPS = 2 * BINS * SAMPLES * FEATURES * CLASSES


def tile_gmpahead_pb_kernel(tc, emb, gamma, beta, fc1d, out):
    nc = tc.nc

    with ExitStack() as ctx:
        keep = ctx.enter_context(tc.tile_pool(name="keep", bufs=1))
        work = ctx.enter_context(tc.tile_pool(name="work", bufs=2))
        psum = ctx.enter_context(tc.psum_pool(name="psum", bufs=1))
        ctx.enter_context(tc.manual_schedule())

        ident_f32 = keep.tile([P, P], F32)
        make_identity(nc, ident_f32[:])

        gain_rows = keep.tile([P, FEATURES], BF16)
        gamma_beta = keep.tile([P, P, PACK], F32)
        emb_sb = keep.tile([P, BINS, FEATURES], BF16)
        fc_sb = keep.tile([P, BINS, PACK, CLASSES], BF16)
        fc_words = fc_sb[:].bitcast(F32)
        nc.vector.memset(gain_rows[:], 0.0)

        def emb_load(n0, n1):
            nc.sync.dma_start(out=emb_sb[:, n0:n1, :], in_=emb[n0:n1].rearrange("n b o -> b n o"))

        def fc_load(n):
            nc.sync.dma_start(
                out=fc_sb[:, n].rearrange("p t k -> p (t k)"), in_=fc1d[n].rearrange("(p t) k -> p (t k)", t=PACK)
            )

        emb_load(0, 2)
        fc_load(0)
        nc.sync.dma_start(out=gain_rows[0:BINS, :], in_=gamma)
        nc.sync.dma_start(out=gain_rows[BETA_ROW : BETA_ROW + BINS, :], in_=beta)
        emb_load(2, 4)
        fc_load(1)
        emb_load(4, 8)
        for n in range(2, BINS):
            fc_load(n)
            if n % 4 == 3 and n + 5 < BINS:
                emb_load(n + 5, min(n + 9, BINS))

        def features_to_partitions(dst, rows):
            by_u = rows.bitcast(F32).rearrange("r (p u) -> r u p", u=PAIR)
            for u in range(PAIR):
                nc.tensor.transpose(dst[:, u, :], by_u[:, u, :], ident_f32[:])

        def load_gains():
            gain_t = psum.tile([P, PAIR, PAIR, P], F32, tag="per_class")
            features_to_partitions(gain_t[:, 0], gain_rows[:])
            nc.vector.tensor_copy(
                out=gamma_beta[:].rearrange("p r (u e) -> p r u e", e=PAIR),
                in_=gain_t[:, 0].bitcast(BF16).rearrange("p u (r e) -> p r u e", e=PAIR),
            )

        x_tiles = {}
        stats_tiles = {}
        rstds = {}
        gains = {}
        shifts = {}
        bn_tiles = {}
        squares_tiles = {}
        sums_tiles = {}
        sample_sums = {}
        above_tiles = {}
        sample_rnorms = {}
        rnorm_tiles = {}
        rnorm_copies = {}
        grouped_tiles = {}
        emb_codes = {}
        emb_scales = {}

        def on_gpsimd(n):
            return True

        def pair_bins(i):
            return min(PAIR, BINS - PAIR * i)

        def emb_statistics(n):
            i, j = divmod(n, PAIR)
            if j == 0:
                x_t = psum.tile([P, PAIR, PAIR, SAMPLES], F32, bufs=2)
                x_tiles[i] = x_t
                stats = work.tile([P, PAIR, PAIR, PAIR, 3], F32, bufs=3)
                stats_tiles[i] = stats
                for k in range(pair_bins(i)):
                    features_to_partitions(x_t[:, k], emb_sb[:, n + k, :])
            for u in range(PAIR):
                nc.vector.bn_stats(
                    out=stats_tiles[i][:, j, u].rearrange("p e s -> p (e s)"),
                    in_=x_tiles[i][:, j, u, :].bitcast(BF16),
                )

        def emb_rstd(i):
            cols = pair_bins(i) * PACK
            by_feature = stats_tiles[i][:].rearrange("p j u e s -> p (j u e) s")
            rstd = work.tile([P, PAIR * PACK], F32)
            nc.scalar.activation(
                out=rstd[:, :cols],
                in_=by_feature[:, :cols, 2],
                func=ACT.Abs_reciprocal_sqrt,
                scale=1.0 / SAMPLES,
                bias=BN_EPS,
            )
            rstds[i] = rstd

        def emb_gains(i):
            n0, gn = PAIR * i, pair_bins(i)
            cols = gn * PACK
            means = stats_tiles[i][:].rearrange("p j u e s -> p (j u e) s")[:, :cols, 1]
            gain = work.tile([P, PAIR * PACK], F32, bufs=3)
            nc.gpsimd.tensor_tensor(
                out=gain[:, :cols],
                in0=gamma_beta[:, n0 : n0 + gn, :].rearrange("p n t -> p (n t)"),
                in1=rstds[i][:, :cols],
                op=ALU.mult,
            )
            mean_gain = work.tile([P, PAIR * PACK], F32)
            nc.gpsimd.tensor_tensor(out=mean_gain[:, :cols], in0=means, in1=gain[:, :cols], op=ALU.mult)
            shift = work.tile([P, PAIR * PACK], F32, bufs=3)
            nc.gpsimd.tensor_tensor(
                out=shift[:, :cols],
                in0=gamma_beta[:, BETA_ROW + n0 : BETA_ROW + n0 + gn, :].rearrange("p n t -> p (n t)"),
                in1=mean_gain[:, :cols],
                op=ALU.subtract,
            )
            gains[i] = gain
            shifts[i] = shift

        def emb_batch_norm(n):
            i, j = divmod(n, PAIR)
            bn_t = work.tile([P, PACK, SAMPLES], F32, bufs=8)
            bn_tiles[n] = bn_t
            x_bf = x_tiles[i][:, j].bitcast(BF16).rearrange("p u (b e) -> p u b e", e=PAIR)
            for t in range(PACK):
                col = j * PACK + t
                x_col = x_bf[:, t // PAIR, :, t % PAIR]
                gain, shift = gains[i][:, col : col + 1], shifts[i][:, col : col + 1]
                if n % 2 == 1:
                    nc.vector.tensor_scalar(
                        out=bn_t[:, t, :], in0=x_col, scalar1=gain, scalar2=shift, op0=ALU.mult, op1=ALU.add
                    )
                else:
                    nc.scalar.activation(out=bn_t[:, t, :], in_=x_col, func=ACT.Identity, scale=gain, bias=shift)

        def emb_squares(n):
            squares = work.tile([P, PACK, SAMPLES], F32, bufs=3)
            squares_tiles[n] = squares
            nc.gpsimd.tensor_tensor(out=squares[:], in0=bn_tiles[n][:], in1=bn_tiles[n][:], op=ALU.mult)

        def emb_sums(n):
            i, j = divmod(n, PAIR)
            if j == 0:
                sums_t = psum.tile([P, PAIR, P], F32, tag="per_sample", bufs=2)
                sums_tiles[i] = sums_t
            for t in range(PACK):
                nc.tensor.matmul(
                    out=sums_tiles[i][:, j, :],
                    lhsT=squares_tiles[n][:, t, :],
                    rhs=ident_f32[:],
                    is_transpose=True,
                    start=(t == 0),
                    stop=(t == PACK - 1),
                )

        def emb_finish_sums(n):
            i, j = divmod(n, PAIR)
            if j == 0:
                sum_sq = work.tile([P, PAIR], F32, tag="sample_sum_sq", bufs=3)
                sample_sums[i] = sum_sq
            unused = work.tile([P, P], F32, tag="unused_sums")
            nc.scalar.activation(
                out=unused[:], in_=sums_tiles[i][:, j, :], func=ACT.Identity, accum_out=sample_sums[i][:, j : j + 1]
            )

        def emb_norm_clamp(i):
            gn = pair_bins(i)
            above = work.tile([P, PAIR], F32)
            nc.scalar.activation(out=above[:, :gn], in_=sample_sums[i][:, :gn], func=ACT.Relu, bias=-L2_EPS_SQUARED)
            above_tiles[i] = above

        def emb_sample_norms(i):
            gn = pair_bins(i)
            above = above_tiles[i]
            rnorm = work.tile([P, PAIR], F32, tag="sample_rnorm")
            nc.scalar.activation(
                out=rnorm[:, :gn], in_=above[:, :gn], func=ACT.Abs_reciprocal_sqrt, bias=L2_EPS_SQUARED
            )
            sample_rnorms[i] = rnorm

        def emb_broadcast(i):
            rnorm_all = psum.tile([P, PAIR, SAMPLES], F32, tag="per_sample", bufs=2)
            rnorm_tiles[i] = rnorm_all
            for j in range(pair_bins(i)):
                nc.tensor.transpose(
                    rnorm_all[:, j, :], sample_rnorms[i][:, j : j + 1].to_broadcast([P, P]), ident_f32[:]
                )

        def emb_rnorm_copy(n):
            if on_gpsimd(n):
                i, j = divmod(n, PAIR)
                rnorm_sb = work.tile([P, SAMPLES], F32, bufs=2)
                nc.scalar.copy(out=rnorm_sb[:], in_=rnorm_tiles[i][:, j, :])
                rnorm_copies[n] = rnorm_sb

        def emb_scale(n):
            i, j = divmod(n, PAIR)
            if j == 0:
                grouped = work.tile([P, PAIR, SAMPLES, PACK], BF16, align_bytes=64, tag="emb_grouped", bufs=2)
                grouped_tiles[i] = grouped
            runs = SAMPLES // RUN
            engine = nc.gpsimd if on_gpsimd(n) else nc.vector
            rnorm = rnorm_copies[n][:] if on_gpsimd(n) else rnorm_tiles[i][:, j]
            engine.tensor_tensor(
                out=grouped_tiles[i][:, j].rearrange("p (r i) t -> p r t i", i=RUN),
                in0=bn_tiles[n][:].rearrange("p t (r i) -> p r t i", i=RUN),
                in1=rnorm.rearrange("p (r i) -> p r i", i=RUN).unsqueeze(2).to_broadcast([P, runs, PACK, RUN]),
                op=ALU.mult,
            )

        def emb_quantise(i):
            gn = pair_bins(i)
            pair_codes = work.tile([P, PAIR, SAMPLES], U32, align_bytes=64, bufs=4)
            pair_scales = work.tile([P, PAIR, SAMPLES], U8, align_bytes=64, bufs=4)
            nc.vector.quantize_mx(
                out=pair_codes[:, :gn].rearrange("p j b -> p (j b)").bitcast(FP8X4),
                scales=pair_scales[:, :gn].rearrange("p j b -> p (j b)"),
                in_=grouped_tiles[i][:, :gn].rearrange("p j b t -> p (j b t)"),
            )
            emb_codes[i] = pair_codes
            emb_scales[i] = pair_scales

        fc_transposed = {}
        class_sums = {}
        class_clamped = {}
        class_rnorms = {}
        rnorm_alls = {}
        fc_grouped = {}
        codes = {}
        scales = {}
        logits_tiles = {}
        stores = {}

        def fc_transpose(n):
            for h in range(HALVES):
                fc_t = psum.tile([P, PACK, P], F32, bufs=2)
                fc_transposed[(n, h)] = fc_t
                for t in range(PACK):
                    nc.tensor.transpose(fc_t[:, t, :], fc_words[:, n, t, h * P : (h + 1) * P], ident_f32[:])

        def fc_squares(n, h):
            if h == 0:
                sum_sq = work.tile([P, NORMS], F32, tag="class_sum_sq", bufs=4)
                class_sums[n] = sum_sq
            by_class = fc_transposed[(n, h)][:].bitcast(BF16).rearrange("k t (p e) -> k t p e", e=PAIR)
            for e in range(PAIR):
                unused = work.tile([P, PACK, P], BF16)
                col = h * PAIR + e
                nc.scalar.activation(
                    out=unused[:],
                    in_=by_class[:, :, :, e],
                    func=ACT.Square,
                    accum_out=class_sums[n][:, col : col + 1],
                )

        def fc_clamp(n):
            clamped = work.tile([P, NORMS], F32, tag="class_clamped", bufs=4)
            nc.scalar.activation(out=clamped[:], in_=class_sums[n][:], func=ACT.Relu, bias=-L2_EPS_SQUARED)
            class_clamped[n] = clamped

        def fc_rnorm(n):
            rnorm = work.tile([P, NORMS], F32, tag="class_rnorm", bufs=4)
            nc.scalar.activation(out=rnorm[:], in_=class_clamped[n][:], func=ACT.Abs_reciprocal_sqrt, bias=L2_EPS_SQUARED)
            class_rnorms[n] = rnorm

        def fc_broadcast(n):
            rnorm_all = psum.tile([P, HALVES, PAIR, P], F32, tag="per_class")
            rnorm_alls[n] = rnorm_all
            for h in range(HALVES):
                for e in range(PAIR):
                    col = h * PAIR + e
                    nc.tensor.transpose(
                        rnorm_all[:, h, e, :], class_rnorms[n][:, col : col + 1].to_broadcast([P, P]), ident_f32[:]
                    )

        def fc_scale(n):
            grouped = work.tile([P, CLASSES, PACK], BF16, align_bytes=64, tag="fc_grouped", bufs=3)
            fc_grouped[n] = grouped
            for h in range(HALVES):
                block = slice(h * P * PAIR, (h + 1) * P * PAIR)
                nc.vector.tensor_tensor(
                    out=grouped[:, block, :].rearrange("p (k e) t -> p k t e", e=PAIR),
                    in0=fc_sb[:, n, :, block].rearrange("p t (k e) -> p k t e", e=PAIR),
                    in1=rnorm_alls[n][:, h].rearrange("p e k -> p k e").unsqueeze(2).to_broadcast([P, P, PACK, PAIR]),
                    op=ALU.mult,
                )

        def fc_quantise(n):
            fc_codes = work.tile([P, CLASSES], U32, align_bytes=64, bufs=5)
            fc_scales = work.tile([P, CLASSES], U8, align_bytes=64, bufs=5)
            nc.vector.quantize_mx(
                out=fc_codes[:].bitcast(FP8X4),
                scales=fc_scales[:],
                in_=fc_grouped[n][:].rearrange("p k t -> p (k t)"),
            )
            codes[n] = fc_codes
            scales[n] = fc_scales

        def multiply(n):
            i, j = divmod(n, PAIR)
            if n >= BINS - LAST:
                logits = psum.tile([P, CLASSES], F32, tag="x_t", bufs=2)
            else:
                logits = psum.tile([P, CLASSES], F32)
            logits_tiles[n] = logits
            nc.tensor.matmul_mx(
                out=logits[:],
                lhsT=emb_codes[i][:, j, :].bitcast(FP8X4),
                lhsT_scale=emb_scales[i][:, j, :],
                rhs=codes[n][:].bitcast(FP8X4),
                rhs_scale=scales[n][:],
                start=True,
                stop=True,
            )

        def copy_and_store(n):
            slot = n % STORE_BINS
            if slot == 0:
                staged = work.tile([P, STORE_BINS, CLASSES], F32, bufs=3)
                stores[n // STORE_BINS] = staged
            staged = stores[n // STORE_BINS]
            if n >= BINS - LAST and n % 2 == 1:
                nc.vector.tensor_copy(out=staged[:, slot, :], in_=logits_tiles[n][:])
            else:
                nc.scalar.copy(out=staged[:, slot, :], in_=logits_tiles[n][:])
            if slot == STORE_BINS - 1 or n == BINS - 1:
                nc.sync.dma_start(out=out[:, n - slot : n + 1, :], in_=staged[:, : slot + 1, :])

        def for_pair(tick, phase, work_on_pair):
            i, odd = divmod(tick - phase + EMB_AHEAD, PAIR)
            if odd == 0 and 0 <= i and PAIR * i < BINS:
                work_on_pair(i)

        def for_bin(tick, phase, work_on_bin):
            n = tick - phase + EMB_AHEAD
            if 0 <= n < BINS:
                work_on_bin(n)

        def for_class_bin(n, work_on_bin):
            if 0 <= n < BINS:
                work_on_bin(n)

        def tick_part(tick, part):
            if part == 0:
                for_bin(tick, 0, emb_statistics)
                for_bin(tick, 4, emb_finish_sums)
                for_pair(tick, 5, emb_norm_clamp)
            if part == 1:
                for_pair(tick, 8, emb_quantise)
                for_pair(tick, 5, emb_sample_norms)
                for_bin(tick, 6, emb_rnorm_copy)
                for_bin(tick, 6, emb_scale)
            if part == 2:
                for_bin(tick, 2, emb_batch_norm)
                for_pair(tick, 1, emb_rstd)
                for_pair(tick, 1, emb_gains)
                for_bin(tick, 2, emb_squares)
            if part == 3:
                for_bin(tick, 3, emb_sums)
                for_pair(tick, 5, emb_broadcast)

        tick = -EMB_AHEAD
        unstored = []
        next_bin = 0
        for step in range(-FC_AHEAD, BINS + 1 + EMB_LAG):
            for n in unstored:
                copy_and_store(n)
            unstored = []
            for_class_bin(step + 2, fc_clamp)
            for catch_up in range(min(1, step - EMB_LAG - tick)):
                for part in range(4):
                    tick_part(tick, part)
                tick += 1
            tick_part(tick, 0)
            for_class_bin(step + 1, fc_quantise)
            for_class_bin(step + 2, fc_rnorm)
            tick_part(tick, 1)
            for_class_bin(step + 3, fc_transpose)
            if step == -FC_AHEAD:
                load_gains()
            for_class_bin(step + 2, fc_broadcast)
            tick_part(tick, 2)
            while next_bin <= min(step - EMB_LAG, BINS - 1) and next_bin in codes and next_bin // PAIR in emb_codes:
                for n in unstored:
                    copy_and_store(n)
                multiply(next_bin)
                unstored = [next_bin]
                next_bin += 1
            if step + 3 < BINS:
                fc_squares(step + 3, 0)
            tick_part(tick, 3)
            if step + 3 < BINS:
                fc_squares(step + 3, 1)
            tick += 1
            for_class_bin(step + 2, fc_scale)
        for n in unstored:
            copy_and_store(n)
